import numpy as np
import ml_dtypes


def mxq(x, axis, fmt="e4m3"):
    dtype, down = {"e4m3": (ml_dtypes.float8_e4m3fn, 7), "e5m2": (ml_dtypes.float8_e5m2, 14)}[fmt]
    v = np.moveaxis(np.asarray(x, np.float32).astype(ml_dtypes.bfloat16).astype(np.float64), axis, -1)
    blocks = v.reshape(v.shape[:-1] + (-1, 32))
    amax = np.abs(blocks).max(-1, keepdims=True)
    byte = np.maximum(np.where(amax > 0, np.frexp(amax)[1] - 1 + 127, 0) - down, 1)
    scale = np.exp2(byte - 127.0)
    codes = (blocks / scale).astype(np.float32).astype(dtype).astype(np.float64)
    return np.moveaxis((codes * scale).reshape(v.shape), -1, axis)


WIDE = False


def mx_kscale(k):
    if not WIDE:
        return np.ones(k)
    levels = np.array([10, -10, 5, -5, 0])
    if k % 512:
        return np.exp2(np.random.permutation(np.resize(levels, k // 32))).repeat(32)
    a = np.empty((k // 512, 16))
    for p in range(k // 512):
        a[p, :8] = np.random.permutation(np.resize(levels, 8))
        for g in range(8):
            far = levels[np.abs(levels - a[p, g]) >= 10]
            a[p, g + 8] = far[np.random.randint(len(far))]
    return np.exp2(a.ravel()).repeat(32)


BF16 = ml_dtypes.bfloat16


def bf(x):
    return np.asarray(x, np.float32).astype(BF16)


def f64(x):
    return np.asarray(x).astype(np.float64)


B, H, FEAT, AUX, NS, FC, C = 4096, 512, 128, 128, 2, 1024, 256
IN = FEAT + AUX + NS


def sigmoid(v):
    return 1.0 / (1.0 + np.exp(-v))


def setup_inputs():
    s = mx_kscale(H)
    s = s / s.max()
    col = np.concatenate([np.full(FEAT, 0.6 / np.sqrt(FEAT)), np.full(AUX, 0.6 / np.sqrt(AUX)), np.full(NS, 0.6 / np.sqrt(NS))])
    return {"x": bf(np.random.standard_normal((B, NS))),
            "feat": bf(np.random.standard_normal((B, FEAT))),
            "aux1": bf(np.random.standard_normal((B, AUX))),
            "h": bf(np.random.standard_normal((B, H)) * s),
            "w_ih": bf(np.random.standard_normal((3 * H, IN)) * col),
            "w_hh": bf(np.random.standard_normal((3 * H, H)) / np.sqrt(H) / s),
            "b_ih": bf(np.random.standard_normal(3 * H) * 0.3),
            "b_hh": bf(np.random.standard_normal(3 * H) * 0.3)}


def reference(x, feat, aux1, h, w_ih, w_hh, b_ih, b_hh):
    hh, wi, xx = f64(h), f64(w_ih), f64(x)
    gi = f64(feat) @ wi[:, :FEAT].T + f64(aux1) @ wi[:, FEAT:FEAT + AUX].T
    for j in range(NS):
        gi = gi + xx[:, j:j + 1] * wi[:, FEAT + AUX + j][None, :]
    gi = gi + f64(b_ih)
    gh = (mxq(hh, 1, "e4m3") @ mxq(f64(w_hh), 1, "e4m3").T) + f64(b_hh)
    i_r, i_z, i_n = np.split(gi, 3, axis=1)
    h_r, h_z, h_n = np.split(gh, 3, axis=1)
    r = sigmoid(i_r + h_r)
    z = sigmoid(i_z + h_z)
    n = np.tanh(i_n + r * h_n)
    return (1.0 - z) * n + z * hh

@@ -1,0 +1,346 @@
+from contextlib import ExitStack
+
+import concourse.mybir as mybir
+from concourse.masks import make_identity
+
+F32 = mybir.dt.float32
+BF16 = mybir.dt.bfloat16
+U32 = mybir.dt.uint32
+U8 = mybir.dt.uint8
+FP8X4 = mybir.dt.float8_e4m3fn_x4
+ALU = mybir.AluOpType
+ACT = mybir.ActivationFunctionType
+
+P = 128
+B = 4096
+H = 512
+IN = 258
+BB = 512
+NBLK = B // BB
+NUNIT = NBLK * 4
+NPAIR = NUNIT // 2
+WROW = 528
+FLOPS = 2 * B * 3 * H * (H + IN)
+PIN = True
+ACC = True
+OUT_LAG = 4
+
+
+def tile_wavernncell_pa_t_kernel(tc, x, feat, aux1, h, w_ih, w_hh, b_ih, b_hh, out):
+    nc = tc.nc
+    with ExitStack() as ctx:
+        const = ctx.enter_context(tc.tile_pool(name="const", bufs=1))
+        ld = ctx.enter_context(tc.tile_pool(name="ld", bufs=3))
+        stage = ctx.enter_context(tc.tile_pool(name="stage", bufs=2))
+        ew = ctx.enter_context(tc.tile_pool(name="ew", bufs=2))
+        outp = ctx.enter_context(tc.tile_pool(name="outp", bufs=4))
+        psum = ctx.enter_context(tc.psum_pool(name="psum", bufs=3))
+        if PIN:
+            ctx.enter_context(tc.manual_schedule())
+
+        xf = x.rearrange("b i -> (b i)")
+        whh_v = w_hh.rearrange("(g m u e) k -> m g u (e k)", g=3, u=2, m=P, e=2)
+        wih_v = w_ih.rearrange("(g m u e) k -> m g u (e k)", g=3, u=2, m=P, e=2)
+
+        warm = const.tile([P, 1], F32, name="warm")
+        nc.vector.memset(warm[:], 0.0)
+        nc.scalar.activation(out=warm[:], in_=warm[:], func=ACT.Sigmoid)
+        ident_f = const.tile([P, P], F32, name="ident_f")
+        make_identity(nc, ident_f[:])
+        ident_b = const.tile([P, P], BF16, name="ident_b")
+        make_identity(nc, ident_b[:])
+        brow = const.tile([P, 512], BF16, name="brow")
+        nc.vector.memset(brow[:], 0.0)
+        t4 = const.tile([P, 4, P], BF16, name="t4")
+        nc.vector.memset(t4[:], 0.0)
+        xm = const.tile([P, 2 * B], BF16, name="xm")
+        nc.vector.memset(xm[:], 0.0)
+
+        whh_sb = const.tile([P, 3, 2, 1024], BF16, name="whh_sb")
+        wih_sb = const.tile([P, 3, 2, WROW], BF16, name="wih_sb")
+        wgrp = const.tile([P, 12 * 512], BF16, name="wgrp", align_bytes=64)
+        wc = const.tile([P, 12 * P], U32, name="wc", align_bytes=64)
+        wsc = const.tile([P, 12 * P], U8, name="wsc", align_bytes=64)
+        wiht = const.tile([P, 2, 12, P], BF16, name="wiht")
+        wx = const.tile([P, 3, 2, 2, 2], F32, name="wx")
+        xw = const.tile([P, 4, P], BF16, name="xw")
+        bias = const.tile([P, 24], F32, name="bias")
+        brz = const.tile([P, 8], F32, name="brz")
+        xs = const.tile([P, B // P, 2], BF16, name="xs")
+
+        whh_w = whh_sb[:].bitcast(F32)
+        wih_w = wih_sb[:].bitcast(F32)
+        wih5 = wih_sb[:, :, :, 0:516].rearrange("m g u (e k) -> m g u e k", e=2)
+        wgrp_w = wgrp[:].bitcast(F32)
+        xmv = xm[:].rearrange("p (b i) -> p b i", i=2)
+
+        loaded = {}
+        staged = {}
+        tags = ["tp", "gi", "gh"]
+        turn = [0]
+
+        def any_bank(shape, dtype):
+            turn[0] += 1
+            return psum.tile(shape, dtype, tag=tags[turn[0] % 3], name="ps_pro", bufs=(3 if turn[0] % 3 == 2 else 2))
+
+        def load(blk):
+            h_sb = ld.tile([P, 4, H], BF16, tag="h", name="h_sb")
+            nc.sync.dma_start(out=h_sb[:], in_=h[blk * BB:(blk + 1) * BB, :].rearrange("(s p) k -> p s k", p=P))
+            cat = ld.tile([P, 4, 256], BF16, tag="cat", name="cat")
+            nc.sync.dma_start(out=cat[:, :, 0:128], in_=feat[blk * BB:(blk + 1) * BB, :].rearrange("(s p) k -> p s k", p=P))
+            nc.sync.dma_start(out=cat[:, :, 128:256], in_=aux1[blk * BB:(blk + 1) * BB, :].rearrange("(s p) k -> p s k", p=P))
+            xb = ld.tile([P, 2 * BB], BF16, tag="xb", name="xb")
+            nc.sync.dma_start(out=xb[:], in_=xf[blk * 2 * BB:(blk + 1) * 2 * BB].partition_broadcast(P))
+            loaded[blk] = (h_sb, cat, xb)
+
+        def stage_h_t(blk, half, ps):
+            if half == 0:
+                hgrp = stage.tile([P, 4 * BB], BF16, tag="hgrp", name="hgrp", bufs=3, align_bytes=64)
+                staged[blk] = [hgrp, None, None, None]
+            hw = loaded[blk][0][:].bitcast(F32)
+            for s2 in range(2):
+                for uu in range(2):
+                    nc.tensor.transpose(ps[:, uu, s2, :], hw[:, half * 2 + s2, uu:256:2], ident_f[:])
+
+        def stage_h_c(blk, half, ps):
+            dst = staged[blk][0][:].bitcast(F32)[:, half * 512:(half + 1) * 512].rearrange("p (b u) -> p b u", u=2)
+            nc.scalar.copy(out=dst, in_=ps[:].rearrange("p u s b -> p (s b) u"))
+
+        def stage_cat_t(blk, ps):
+            cw = loaded[blk][1][:].bitcast(F32)
+            for s in range(4):
+                nc.tensor.transpose(ps[:, s // 2, s % 2, :], cw[:, s, :], ident_f[:])
+
+        def stage_cat_c(blk, ps):
+            catt = stage.tile([P, BB], F32, tag="catt", name="catt")
+            nc.scalar.copy(out=catt[:], in_=ps[:].rearrange("p a s b -> p (a s b)"))
+            staged[blk][3] = catt
+
+        def x1_bank(blk):
+            px = psum.tile([P, BB], BF16, tag="px", name="px", bufs=1)
+            for s in range(4):
+                nc.tensor.transpose(px[:, s * P:(s + 1) * P], xs[:, blk * 4 + s, 1:2].to_broadcast([P, P]), ident_b[:])
+            staged[blk].append(px)
+
+        def stage_q(blk):
+            hc = stage.tile([P, BB], U32, tag="hc", name="hc", align_bytes=64)
+            hs = stage.tile([P, BB], U8, tag="hs", name="hs", align_bytes=64)
+            nc.vector.quantize_mx(out=hc[:].bitcast(FP8X4), scales=hs[:], in_=staged[blk][0][:])
+            staged[blk][1] = hc
+            staged[blk][2] = hs
+
+        def quant_w(gu):
+            nc.vector.quantize_mx(
+                out=wc[:, gu * 256:(gu + 1) * 256].bitcast(FP8X4),
+                scales=wsc[:, gu * 256:(gu + 1) * 256],
+                in_=wgrp[:, gu * 1024:(gu + 1) * 1024],
+            )
+
+        def prep_w(u):
+            for g in range(3):
+                gu = g * 2 + u
+                ps = any_bank([P, 2, 2, P], F32)
+                for e in range(2):
+                    for uu in range(2):
+                        nc.tensor.transpose(ps[:, uu, e, :], whh_w[:, g, u, e * 256 + uu:(e + 1) * 256:2], ident_f[:])
+                dst = wgrp_w[:, gu * 512:(gu + 1) * 512].rearrange("p (e m k) -> p e m k", e=2, k=2)
+                nc.vector.tensor_copy(out=dst, in_=ps[:].rearrange("p k e m -> p e m k"))
+                if g > 0:
+                    quant_w(gu - 2)
+            for g in range(3):
+                gu = g * 2 + u
+                ps2 = any_bank([P, 2, P], F32)
+                for e in range(2):
+                    nc.tensor.transpose(ps2[:, e, :], wih_w[:, g, u, e * 129:e * 129 + P], ident_f[:])
+                src = ps2[:].bitcast(BF16).rearrange("w e (m k) -> w k e m", k=2)
+                nc.scalar.copy(out=wiht[:, :, gu * 2:gu * 2 + 2, :], in_=src)
+            quant_w(4 + u)
+            nc.vector.tensor_copy(out=wx[:, :, u, :, :], in_=wih5[:, :, u, :, 256:258])
+            nc.vector.tensor_copy(out=t4[:, u * 2:u * 2 + 2, 0:2], in_=wih5[:, 2, u, :, 256:258])
+
+        nc.sync.dma_start(out=whh_sb[:, :, 0, :], in_=whh_v[:, :, 0, :])
+        nc.sync.dma_start(out=wih_sb[:, :, 0, 0:516], in_=wih_v[:, :, 0, :])
+        nc.sync.dma_start(out=whh_sb[:, :, 1, :], in_=whh_v[:, :, 1, :])
+        nc.sync.dma_start(out=wih_sb[:, :, 1, 0:516], in_=wih_v[:, :, 1, :])
+        load(0)
+        nc.sync.dma_start(out=xs[:], in_=x.rearrange("(t p) i -> p t i", p=P))
+        nc.sync.dma_start(out=brow[0:3, :], in_=b_ih.rearrange("(r c) -> r c", c=512))
+        nc.sync.dma_start(out=brow[3:6, :], in_=b_hh.rearrange("(r c) -> r c", c=512))
+        nc.sync.dma_start(out=xm[0:1, :], in_=xf.unsqueeze(0))
+        nc.sync.dma_start(out=xm[1:2, 0:2 * B - 1], in_=xf[1:2 * B].unsqueeze(0))
+        load(1)
+
+        prep_w(0)
+        prep_w(1)
+        psx = any_bank([P, 4, P], BF16)
+        for c in range(4):
+            nc.tensor.transpose(psx[:, c, :], t4[:, c, :], ident_b[:])
+        nc.vector.tensor_copy(out=xw[:], in_=psx[:])
+        for half in range(2):
+            ps = any_bank([P, 2, 2, P], F32)
+            stage_h_t(0, half, ps)
+            stage_h_c(0, half, ps)
+        ps = any_bank([P, 2, 2, P], F32)
+        stage_cat_t(0, ps)
+        stage_cat_c(0, ps)
+        psb = any_bank([P, 2, P], F32)
+        for uu in range(2):
+            nc.tensor.transpose(psb[:, uu, :], brow[:].bitcast(F32)[:, uu:256:2], ident_f[:])
+        for uu in range(2):
+            dst = bias[:].rearrange("p (r u e) -> p r u e", u=2, e=2)[:, :, uu, :]
+            nc.vector.tensor_copy(out=dst, in_=psb[:, uu, 0:6].bitcast(BF16).rearrange("p (r e) -> p r e", e=2))
+        nc.vector.tensor_tensor(out=brz[:], in0=bias[:, 0:8], in1=bias[:, 12:20], op=ALU.add)
+        stage_q(0)
+        x1_bank(0)
+
+        pairs = {}
+        units = {}
+        obs = {}
+
+        def mm_mx(i, g):
+            blk, c = divmod(i, 4)
+            q = g * 4 + c
+            gh = psum.tile([P, BB], F32, tag="gh", name="gh")
+            nc.tensor.matmul_mx(
+                out=gh[:],
+                lhsT=wc[:, q * P:(q + 1) * P].bitcast(FP8X4),
+                lhsT_scale=wsc[:, q * P:(q + 1) * P],
+                rhs=staged[blk][1][:].bitcast(FP8X4),
+                rhs_scale=staged[blk][2][:],
+                start=True,
+                stop=True,
+            )
+            return gh
+
+        def mm_plain(i, g):
+            blk, c = divmod(i, 4)
+            q = g * 4 + c
+            cb = staged[blk][3][:].bitcast(BF16).rearrange("p (b e) -> p b e", e=2)
+            gi = psum.tile([P, BB], F32, tag="gi", name="gi", bufs=2)
+            nc.tensor.matmul(gi[:], lhsT=wiht[:, 0, q, :], rhs=cb[:, :, 0], start=True, stop=False)
+            nc.tensor.matmul(gi[:], lhsT=wiht[:, 1, q, :], rhs=cb[:, :, 1], start=False, stop=(g < 2))
+            if g == 2:
+                nc.tensor.matmul(gi[:], lhsT=xw[:, c, :], rhs=xmv[:, blk * BB:(blk + 1) * BB, 0], start=False, stop=True)
+            return gi
+
+        def x_term(i, g, t, dst, acc):
+            blk, c = divmod(i, 4)
+            xbv = loaded[blk][2][:].rearrange("p (b i) -> p b i", i=2)
+            nc.vector.scalar_tensor_tensor(out=dst, in0=xbv[:, :, t], scalar=wx[:, g, c // 2, c % 2, t:t + 1], in1=acc, op0=ALU.mult, op1=ALU.add)
+
+        def out_t(k, ps):
+            w, sp = divmod(k, 2)
+            dd, nn = pairs[w]["d"], pairs[w]["n"]
+            for s2 in range(2):
+                for e in range(2):
+                    lo = (2 * sp + s2) * P
+                    nc.tensor.matmul(ps[:, s2, e, :], lhsT=dd[:, e, lo:lo + P], rhs=ident_f[:], is_transpose=True, start=True, stop=False)
+                    nc.tensor.matmul(ps[:, s2, e, :], lhsT=nn[:, e, lo:lo + P], rhs=ident_f[:], is_transpose=True, start=False, stop=True)
+
+        def out_c(k, ps, on_vector):
+            w, sp = divmod(k, 2)
+            blk, u = divmod(w, 2)
+            if u == 0:
+                obs[(blk, sp)] = outp.tile([P, 2, 512], F32, tag="ob", name="ob")
+            ob = obs[(blk, sp)]
+            dst = ob[:].rearrange("b s (p t) -> b s p t", t=4)[:, :, :, 2 * u:2 * u + 2]
+            src = ps[:].rearrange("b s e p -> b s p e")
+            if on_vector:
+                nc.vector.tensor_copy(out=dst, in_=src)
+            else:
+                nc.scalar.copy(out=dst, in_=src)
+            if u == 1:
+                r0 = blk * BB + sp * 256
+                nc.sync.dma_start(out=out[r0:r0 + 256, :].rearrange("(s b) j -> b s j", b=P), in_=ob[:])
+
+        for j in range(NUNIT + OUT_LAG):
+            blk, c = divmod(j, 4)
+            u, e = divmod(c, 2)
+            w = j // 2
+            live = j < NUNIT
+            lag = 1 <= j <= NUNIT
+            jn = j - 1
+            cn = jn % 4
+            wn = jn // 2
+            nxt = blk + 1
+            k = j - OUT_LAG
+            if live:
+                if c == 0 and blk + 2 < NBLK:
+                    load(blk + 2)
+                gi_r = mm_plain(j, 0)
+            if lag:
+                gh_n = mm_mx(jn, 2)
+            if live:
+                gi_z = mm_plain(j, 1)
+                gh_r = mm_mx(j, 0)
+            if live:
+                gh_z = mm_mx(j, 1)
+            if lag:
+                gi_n = mm_plain(jn, 2)
+            ps_o = None
+            if 0 <= k:
+                ps_o = psum.tile([P, 2, 2, P], F32, tag="tp", name="ps_o", bufs=2)
+                out_t(k, ps_o)
+            ps_i = None
+            if live and nxt < NBLK and c < 3:
+                ps_i = psum.tile([P, 2, 2, P], F32, tag="tp", name="ps_i", bufs=2)
+                if c < 2:
+                    stage_h_t(nxt, c, ps_i)
+                else:
+                    stage_cat_t(nxt, ps_i)
+            if live:
+                if e == 0:
+                    pairs[w] = {
+                        "a1": ew.tile([P, 2, BB], F32, tag="az1", name="az1"),
+                        "a2": ew.tile([P, 2, BB], F32, tag="az2", name="az2"),
+                        "n": ew.tile([P, 2, BB], F32, tag="n", name="n", bufs=3),
+                    }
+                pw = pairs[w]
+                a1 = ew.tile([P, BB], F32, tag="a1", name="a1")
+                x_term(j, 0, 0, a1[:], gi_r[:])
+            if lag:
+                v = ew.tile([P, BB], F32, tag="v", name="v")
+                nc.vector.scalar_tensor_tensor(out=v[:], in0=gh_n[:], scalar=bias[:, 20 + cn:21 + cn], in1=units[jn][:], op0=ALU.add, op1=ALU.mult)
+            if live:
+                nc.vector.scalar_tensor_tensor(out=a1[:], in0=staged[blk][4][:], scalar=wx[:, 0, u, e, 1:2], in1=a1[:], op0=ALU.mult, op1=ALU.add)
+                x_term(j, 1, 0, pw["a1"][:, e, :], gi_z[:])
+                nc.vector.tensor_tensor(out=a1[:], in0=gh_r[:], in1=a1[:], op=ALU.add)
+                r = ew.tile([P, BB], F32, tag="r", name="r")
+                nc.scalar.activation(out=r[:], in_=a1[:], func=ACT.Sigmoid, bias=brz[:, c:c + 1], scale=1.0)
+                units[j] = r
+            if lag:
+                pn = pairs[wn]
+                nc.vector.tensor_tensor(out=v[:], in0=gi_n[:], in1=v[:], op=ALU.add)
+                nc.scalar.activation(out=pn["n"][:, cn % 2, :], in_=v[:], func=ACT.Tanh, bias=bias[:, 8 + cn:9 + cn], scale=1.0)
+                if cn % 2 == 1:
+                    pn["d"] = ew.tile([P, 2, BB], F32, tag="d", name="d", bufs=3)
+                    un = cn // 2
+                    ht = staged[jn // 4][0][:].rearrange("p (b t) -> p t b", t=4)[:, 2 * un:2 * un + 2, :]
+                    eng = nc.vector if wn == NPAIR - 1 else nc.gpsimd
+                    eng.tensor_tensor(out=pn["d"][:], in0=ht, in1=pn["n"][:], op=ALU.subtract)
+            if live:
+                x_term(j, 1, 1, pw["a2"][:, e, :], gh_z[:])
+                if e == 1:
+                    nc.gpsimd.tensor_tensor(out=pw["a1"][:], in0=pw["a1"][:], in1=pw["a2"][:], op=ALU.add)
+            if j % 2 == 0 and 2 <= j <= NUNIT:
+                wp = w - 1
+                pp = pairs[wp]
+                up = wp % 2
+                z = ew.tile([P, 2, BB], F32, tag="z", name="z")
+                for ez in range(2):
+                    cz = 4 + 2 * up + ez
+                    nc.scalar.activation(out=z[:, ez, :], in_=pp["a1"][:, ez, :], func=ACT.Sigmoid, bias=brz[:, cz:cz + 1], scale=1.0)
+                eng = nc.vector if wp == NPAIR - 1 else nc.gpsimd
+                eng.tensor_tensor(out=pp["d"][:], in0=pp["d"][:], in1=z[:], op=ALU.mult)
+            if ps_o is not None:
+                out_c(k, ps_o, (not live) and k % 2 == 1)
+            if ps_i is not None:
+                if c < 2:
+                    stage_h_c(nxt, c, ps_i)
+                else:
+                    stage_cat_c(nxt, ps_i)
+            if live:
+                if c == 2 and nxt < NBLK:
+                    stage_q(nxt)
+                if c == 3 and nxt < NBLK:
+                    x1_bank(nxt)

@@ -17,13 +17,10 @@ H = 512
 IN = 258
 BB = 512
 NBLK = B // BB
-NUNIT = NBLK * 4
-NPAIR = NUNIT // 2
-WROW = 528
+NU = NBLK * 4
+LAG = 5
+WROW = 264
 FLOPS = 2 * B * 3 * H * (H + IN)
-PIN = True
-ACC = True
-OUT_LAG = 4
 
 
 def tile_wavernncell_pa_t_kernel(tc, x, feat, aux1, h, w_ih, w_hh, b_ih, b_hh, out):
@@ -31,16 +28,14 @@ def tile_wavernncell_pa_t_kernel(tc, x, feat, aux1, h, w_ih, w_hh, b_ih, b_hh, o
     with ExitStack() as ctx:
         const = ctx.enter_context(tc.tile_pool(name="const", bufs=1))
         ld = ctx.enter_context(tc.tile_pool(name="ld", bufs=3))
-        stage = ctx.enter_context(tc.tile_pool(name="stage", bufs=2))
-        ew = ctx.enter_context(tc.tile_pool(name="ew", bufs=2))
-        outp = ctx.enter_context(tc.tile_pool(name="outp", bufs=4))
-        psum = ctx.enter_context(tc.psum_pool(name="psum", bufs=3))
-        if PIN:
-            ctx.enter_context(tc.manual_schedule())
+        stage = ctx.enter_context(tc.tile_pool(name="stage", bufs=3))
+        ew = ctx.enter_context(tc.tile_pool(name="ew", bufs=3))
+        psum = ctx.enter_context(tc.psum_pool(name="psum", bufs=7))
+        ctx.enter_context(tc.manual_schedule())
 
         xf = x.rearrange("b i -> (b i)")
-        whh_v = w_hh.rearrange("(g m u e) k -> m g u (e k)", g=3, u=2, m=P, e=2)
-        wih_v = w_ih.rearrange("(g m u e) k -> m g u (e k)", g=3, u=2, m=P, e=2)
+        whh_v = w_hh.rearrange("(g c m) k -> m g c k", g=3, m=P)
+        wih_v = w_ih.rearrange("(g c m) k -> m g c k", g=3, m=P)
 
         warm = const.tile([P, 1], F32, name="warm")
         nc.vector.memset(warm[:], 0.0)
@@ -49,298 +44,314 @@ def tile_wavernncell_pa_t_kernel(tc, x, feat, aux1, h, w_ih, w_hh, b_ih, b_hh, o
         make_identity(nc, ident_f[:])
         ident_b = const.tile([P, P], BF16, name="ident_b")
         make_identity(nc, ident_b[:])
-        brow = const.tile([P, 512], BF16, name="brow")
+        brow = const.tile([P, P], BF16, name="brow")
         nc.vector.memset(brow[:], 0.0)
+        xrow = const.tile([P, 256], BF16, name="xrow")
+        nc.vector.memset(xrow[:], 0.0)
         t4 = const.tile([P, 4, P], BF16, name="t4")
         nc.vector.memset(t4[:], 0.0)
-        xm = const.tile([P, 2 * B], BF16, name="xm")
-        nc.vector.memset(xm[:], 0.0)
+        xt = const.tile([P, B], BF16, name="xt")
+        nc.gpsimd.memset(xt[:], 1.0)
+        xr = const.tile([2, 2 * B], BF16, name="xr")
 
-        whh_sb = const.tile([P, 3, 2, 1024], BF16, name="whh_sb")
-        wih_sb = const.tile([P, 3, 2, WROW], BF16, name="wih_sb")
-        wgrp = const.tile([P, 12 * 512], BF16, name="wgrp", align_bytes=64)
+        whh_sb = const.tile([P, 4, 3, H], BF16, name="whh_sb")
+        wih_sb = const.tile([P, 3, 4, WROW], BF16, name="wih_sb")
         wc = const.tile([P, 12 * P], U32, name="wc", align_bytes=64)
         wsc = const.tile([P, 12 * P], U8, name="wsc", align_bytes=64)
-        wiht = const.tile([P, 2, 12, P], BF16, name="wiht")
-        wx = const.tile([P, 3, 2, 2, 2], F32, name="wx")
-        xw = const.tile([P, 4, P], BF16, name="xw")
+        wt = const.tile([P, 2, 3, H], BF16, name="wt")
+        wz0 = const.tile([P, 4], F32, name="wz0")
+        wz1 = const.tile([P, H], BF16, name="wz1")
+        xw = const.tile([P, H], BF16, name="xw")
         bias = const.tile([P, 24], F32, name="bias")
         brz = const.tile([P, 8], F32, name="brz")
         xs = const.tile([P, B // P, 2], BF16, name="xs")
-
         whh_w = whh_sb[:].bitcast(F32)
         wih_w = wih_sb[:].bitcast(F32)
-        wih5 = wih_sb[:, :, :, 0:516].rearrange("m g u (e k) -> m g u e k", e=2)
-        wgrp_w = wgrp[:].bitcast(F32)
-        xmv = xm[:].rearrange("p (b i) -> p b i", i=2)
 
-        loaded = {}
-        staged = {}
-        tags = ["tp", "gi", "gh"]
-        turn = [0]
+        hs_ = {}
+        cats = {}
+        xbs = {}
+        hgrps = {}
+        codes = {}
+        catts = {}
+        pxs = {}
 
-        def any_bank(shape, dtype):
-            turn[0] += 1
-            return psum.tile(shape, dtype, tag=tags[turn[0] % 3], name="ps_pro", bufs=(3 if turn[0] % 3 == 2 else 2))
+        def bank(shape, dtype=F32):
+            return psum.tile(shape, dtype, tag="ring", name="ring", bufs=7)
 
         def load(blk):
-            h_sb = ld.tile([P, 4, H], BF16, tag="h", name="h_sb")
-            nc.sync.dma_start(out=h_sb[:], in_=h[blk * BB:(blk + 1) * BB, :].rearrange("(s p) k -> p s k", p=P))
-            cat = ld.tile([P, 4, 256], BF16, tag="cat", name="cat")
-            nc.sync.dma_start(out=cat[:, :, 0:128], in_=feat[blk * BB:(blk + 1) * BB, :].rearrange("(s p) k -> p s k", p=P))
-            nc.sync.dma_start(out=cat[:, :, 128:256], in_=aux1[blk * BB:(blk + 1) * BB, :].rearrange("(s p) k -> p s k", p=P))
-            xb = ld.tile([P, 2 * BB], BF16, tag="xb", name="xb")
-            nc.sync.dma_start(out=xb[:], in_=xf[blk * 2 * BB:(blk + 1) * 2 * BB].partition_broadcast(P))
-            loaded[blk] = (h_sb, cat, xb)
+            hs_[blk] = ld.tile([P, 4, H], BF16, tag="h", name="h_sb", bufs=5)
+            nc.sync.dma_start(out=hs_[blk][:], in_=h[blk * BB:(blk + 1) * BB, :].rearrange("(s p) k -> p s k", p=P))
+            cats[blk] = ld.tile([P, 4, 256], BF16, tag="cat", name="cat")
+            nc.sync.dma_start(out=cats[blk][:, :, 0:128], in_=feat[blk * BB:(blk + 1) * BB, :].rearrange("(s p) k -> p s k", p=P))
+            nc.sync.dma_start(out=cats[blk][:, :, 128:256], in_=aux1[blk * BB:(blk + 1) * BB, :].rearrange("(s p) k -> p s k", p=P))
+            xbs[blk] = ld.tile([P, BB, 2], BF16, tag="xb", name="xb")
+            nc.sync.dma_start(out=xbs[blk][:].rearrange("p b i -> p (b i)"), in_=xf[blk * 2 * BB:(blk + 1) * 2 * BB].partition_broadcast(P))
 
-        def stage_h_t(blk, half, ps):
-            if half == 0:
-                hgrp = stage.tile([P, 4 * BB], BF16, tag="hgrp", name="hgrp", bufs=3, align_bytes=64)
-                staged[blk] = [hgrp, None, None, None]
-            hw = loaded[blk][0][:].bitcast(F32)
+        def h_t(blk, half):
+            ps = bank([P, 2, 2, P])
+            hw = hs_[blk][:].bitcast(F32)
             for s2 in range(2):
                 for uu in range(2):
                     nc.tensor.transpose(ps[:, uu, s2, :], hw[:, half * 2 + s2, uu:256:2], ident_f[:])
+            return ps
 
-        def stage_h_c(blk, half, ps):
-            dst = staged[blk][0][:].bitcast(F32)[:, half * 512:(half + 1) * 512].rearrange("p (b u) -> p b u", u=2)
+        def h_c(blk, half, ps):
+            if half == 0:
+                hgrps[blk] = stage.tile([P, 4 * BB], BF16, tag="hgrp", name="hgrp", bufs=2, align_bytes=64)
+            dst = hgrps[blk][:].bitcast(F32)[:, half * 512:(half + 1) * 512].rearrange("p (b u) -> p b u", u=2)
             nc.scalar.copy(out=dst, in_=ps[:].rearrange("p u s b -> p (s b) u"))
 
-        def stage_cat_t(blk, ps):
-            cw = loaded[blk][1][:].bitcast(F32)
+        def h_q(blk):
+            hc = stage.tile([P, BB], U32, tag="hc", name="hc", align_bytes=64)
+            hsc = stage.tile([P, BB], U8, tag="hsc", name="hsc", align_bytes=64)
+            nc.vector.quantize_mx(out=hc[:].bitcast(FP8X4), scales=hsc[:], in_=hgrps[blk][:])
+            codes[blk] = (hc, hsc)
+
+        def cat_t(blk):
+            ps = bank([P, 4, P])
+            cw = cats[blk][:].bitcast(F32)
             for s in range(4):
-                nc.tensor.transpose(ps[:, s // 2, s % 2, :], cw[:, s, :], ident_f[:])
+                nc.tensor.transpose(ps[:, s, :], cw[:, s, :], ident_f[:])
+            return ps
 
-        def stage_cat_c(blk, ps):
-            catt = stage.tile([P, BB], F32, tag="catt", name="catt")
-            nc.scalar.copy(out=catt[:], in_=ps[:].rearrange("p a s b -> p (a s b)"))
-            staged[blk][3] = catt
+        def cat_c(blk, ps):
+            catts[blk] = stage.tile([P, 2, BB], BF16, tag="catt", name="catt")
+            nc.scalar.copy(out=catts[blk][:], in_=ps[:].rearrange("w s b -> w (s b)").bitcast(BF16).rearrange("w (b e) -> w e b", e=2))
 
-        def x1_bank(blk):
+        def px_t(blk):
             px = psum.tile([P, BB], BF16, tag="px", name="px", bufs=1)
             for s in range(4):
                 nc.tensor.transpose(px[:, s * P:(s + 1) * P], xs[:, blk * 4 + s, 1:2].to_broadcast([P, P]), ident_b[:])
-            staged[blk].append(px)
+            pxs[blk] = px
 
-        def stage_q(blk):
-            hc = stage.tile([P, BB], U32, tag="hc", name="hc", align_bytes=64)
-            hs = stage.tile([P, BB], U8, tag="hs", name="hs", align_bytes=64)
-            nc.vector.quantize_mx(out=hc[:].bitcast(FP8X4), scales=hs[:], in_=staged[blk][0][:])
-            staged[blk][1] = hc
-            staged[blk][2] = hs
-
-        def quant_w(gu):
-            nc.vector.quantize_mx(
-                out=wc[:, gu * 256:(gu + 1) * 256].bitcast(FP8X4),
-                scales=wsc[:, gu * 256:(gu + 1) * 256],
-                in_=wgrp[:, gu * 1024:(gu + 1) * 1024],
-            )
-
-        def prep_w(u):
-            for g in range(3):
-                gu = g * 2 + u
-                ps = any_bank([P, 2, 2, P], F32)
-                for e in range(2):
+        def whh_t(c):
+            banks = []
+            for gs in ((0, 1), (2,)):
+                ps = bank([P, len(gs), 2, P])
+                for j, g in enumerate(gs):
                     for uu in range(2):
-                        nc.tensor.transpose(ps[:, uu, e, :], whh_w[:, g, u, e * 256 + uu:(e + 1) * 256:2], ident_f[:])
-                dst = wgrp_w[:, gu * 512:(gu + 1) * 512].rearrange("p (e m k) -> p e m k", e=2, k=2)
-                nc.vector.tensor_copy(out=dst, in_=ps[:].rearrange("p k e m -> p e m k"))
-                if g > 0:
-                    quant_w(gu - 2)
-            for g in range(3):
-                gu = g * 2 + u
-                ps2 = any_bank([P, 2, P], F32)
-                for e in range(2):
-                    nc.tensor.transpose(ps2[:, e, :], wih_w[:, g, u, e * 129:e * 129 + P], ident_f[:])
-                src = ps2[:].bitcast(BF16).rearrange("w e (m k) -> w k e m", k=2)
-                nc.scalar.copy(out=wiht[:, :, gu * 2:gu * 2 + 2, :], in_=src)
-            quant_w(4 + u)
-            nc.vector.tensor_copy(out=wx[:, :, u, :, :], in_=wih5[:, :, u, :, 256:258])
-            nc.vector.tensor_copy(out=t4[:, u * 2:u * 2 + 2, 0:2], in_=wih5[:, 2, u, :, 256:258])
+                        nc.tensor.transpose(ps[:, j, uu, :], whh_w[:, c, g, uu:256:2], ident_f[:])
+                banks.append(ps)
+            return banks
 
-        nc.sync.dma_start(out=whh_sb[:, :, 0, :], in_=whh_v[:, :, 0, :])
-        nc.sync.dma_start(out=wih_sb[:, :, 0, 0:516], in_=wih_v[:, :, 0, :])
-        nc.sync.dma_start(out=whh_sb[:, :, 1, :], in_=whh_v[:, :, 1, :])
-        nc.sync.dma_start(out=wih_sb[:, :, 1, 0:516], in_=wih_v[:, :, 1, :])
-        load(0)
-        nc.sync.dma_start(out=xs[:], in_=x.rearrange("(t p) i -> p t i", p=P))
-        nc.sync.dma_start(out=brow[0:3, :], in_=b_ih.rearrange("(r c) -> r c", c=512))
-        nc.sync.dma_start(out=brow[3:6, :], in_=b_hh.rearrange("(r c) -> r c", c=512))
-        nc.sync.dma_start(out=xm[0:1, :], in_=xf.unsqueeze(0))
-        nc.sync.dma_start(out=xm[1:2, 0:2 * B - 1], in_=xf[1:2 * B].unsqueeze(0))
+        def whh_c(c, banks, engines):
+            grp = stage.tile([P, 3 * H], BF16, tag="wgrp", name="wgrp", bufs=3, align_bytes=64)
+            w = grp[:].bitcast(F32)
+            for j, ps in enumerate(banks):
+                n = 2 - j
+                dst = w[:, j * 512:j * 512 + n * 256].rearrange("p (g m u) -> p g m u", m=P, u=2)
+                src = ps[:].rearrange("p g u m -> p g m u")
+                if engines[j] is nc.scalar:
+                    nc.scalar.copy(out=dst, in_=src)
+                else:
+                    nc.vector.tensor_copy(out=dst, in_=src)
+            return grp
+
+        def whh_q(c, grp):
+            for lo, n in ((0, 2), (2, 1)):
+                a, b = (c * 3 + lo) * P, (c * 3 + lo + n) * P
+                nc.vector.quantize_mx(out=wc[:, a:b].bitcast(FP8X4), scales=wsc[:, a:b], in_=grp[:, lo * H:(lo + n) * H])
+
+        def wih_t(g):
+            ps = bank([P, 4, P])
+            for c in range(4):
+                nc.tensor.transpose(ps[:, c, :], wih_w[:, g, c, 0:P], ident_f[:])
+            return ps
+
+        def wih_c(g, ps, on_scalar):
+            src = ps[:].rearrange("w c m -> w (c m)").bitcast(BF16).rearrange("w (m e) -> w e m", e=2)
+            if on_scalar:
+                nc.scalar.copy(out=wt[:, :, g, :], in_=src)
+            else:
+                nc.vector.tensor_copy(out=wt[:, :, g, :], in_=src)
+
+        nc.sync.dma_start(out=whh_sb[:, 0, :, :], in_=whh_v[:, :, 0, :])
+        hs_[0] = ld.tile([P, 4, H], BF16, tag="h", name="h_sb", bufs=5)
+        nc.sync.dma_start(out=hs_[0][:], in_=h[0:BB, :].rearrange("(s p) k -> p s k", p=P))
+        cats[0] = ld.tile([P, 4, 256], BF16, tag="cat", name="cat")
+        nc.sync.dma_start(out=cats[0][:, :, 0:128], in_=feat[0:BB, :].rearrange("(s p) k -> p s k", p=P))
+        nc.sync.dma_start(out=cats[0][:, :, 128:256], in_=aux1[0:BB, :].rearrange("(s p) k -> p s k", p=P))
+        nc.sync.dma_start(out=wih_sb[:, 0, :, 0:IN], in_=wih_v[:, 0, :, :])
+        nc.scalar.dma_start(out=xrow[0:32, :], in_=xf.rearrange("(t c) -> t c", c=256))
+        nc.scalar.dma_start(out=brow[0:12, :], in_=b_ih.rearrange("(r c) -> r c", c=P))
+        nc.scalar.dma_start(out=brow[12:24, :], in_=b_hh.rearrange("(r c) -> r c", c=P))
+        xbs[0] = ld.tile([P, BB, 2], BF16, tag="xb", name="xb")
+        nc.sync.dma_start(out=xbs[0][:].rearrange("p b i -> p (b i)"), in_=xf[0:2 * BB].partition_broadcast(P))
+        nc.sync.dma_start(out=wih_sb[:, 1, :, 0:IN], in_=wih_v[:, 1, :, :])
+        for c in range(1, 4):
+            nc.sync.dma_start(out=whh_sb[:, c, :, :], in_=whh_v[:, :, c, :])
+        nc.sync.dma_start(out=wih_sb[:, 2, :, 0:IN], in_=wih_v[:, 2, :, :])
+        nc.sync.dma_start(out=xr[0:1, :], in_=xf.unsqueeze(0))
+        nc.sync.dma_start(out=xr[1:2, 0:2 * B - 1], in_=xf[1:2 * B].unsqueeze(0))
         load(1)
 
-        prep_w(0)
-        prep_w(1)
-        psx = any_bank([P, 4, P], BF16)
-        for c in range(4):
-            nc.tensor.transpose(psx[:, c, :], t4[:, c, :], ident_b[:])
-        nc.vector.tensor_copy(out=xw[:], in_=psx[:])
-        for half in range(2):
-            ps = any_bank([P, 2, 2, P], F32)
-            stage_h_t(0, half, ps)
-            stage_h_c(0, half, ps)
-        ps = any_bank([P, 2, 2, P], F32)
-        stage_cat_t(0, ps)
-        stage_cat_c(0, ps)
-        psb = any_bank([P, 2, P], F32)
-        for uu in range(2):
-            nc.tensor.transpose(psb[:, uu, :], brow[:].bitcast(F32)[:, uu:256:2], ident_f[:])
-        for uu in range(2):
-            dst = bias[:].rearrange("p (r u e) -> p r u e", u=2, e=2)[:, :, uu, :]
-            nc.vector.tensor_copy(out=dst, in_=psb[:, uu, 0:6].bitcast(BF16).rearrange("p (r e) -> p r e", e=2))
+        nc.gpsimd.tensor_scalar(out=xt[0:2, :], in0=xr[:, 0:2 * B:2], scalar1=1.0, scalar2=0.0, op0=ALU.mult, op1=ALU.add)
+        banks = whh_t(0)
+        grp = whh_c(0, banks, (nc.vector, nc.scalar))
+        ph0 = h_t(0, 0)
+        ph1 = h_t(0, 1)
+        h_c(0, 0, ph0)
+        h_c(0, 1, ph1)
+        whh_q(0, grp)
+        pc = cat_t(0)
+        cat_c(0, pc)
+        pw = wih_t(0)
+        psx = bank([P, P])
+        nc.tensor.transpose(psx[:], xrow[:].bitcast(F32), ident_f[:])
+        psb = bank([P, P], BF16)
+        nc.tensor.transpose(psb[:], brow[:], ident_b[:])
+        h_q(0)
+        wih_c(0, pw, False)
+        nc.vector.tensor_copy(out=xs[:], in_=psx[:, 0:32].bitcast(BF16).rearrange("p (t i) -> p t i", i=2))
+        nc.vector.tensor_copy(out=bias[:], in_=psb[:, 0:24])
         nc.vector.tensor_tensor(out=brz[:], in0=bias[:, 0:8], in1=bias[:, 12:20], op=ALU.add)
-        stage_q(0)
-        x1_bank(0)
+        nc.vector.tensor_copy(out=wz0[:], in_=wih_sb[:, 1, :, 256:257].rearrange("p c i -> p (c i)"))
+        px_t(0)
+        banks = whh_t(1)
+        grps = {1: whh_c(1, banks, (nc.scalar, nc.scalar))}
 
-        pairs = {}
-        units = {}
-        obs = {}
+        rs = {}
+        late = []
+        zts = {}
+        vs = {}
 
         def mm_mx(i, g):
             blk, c = divmod(i, 4)
-            q = g * 4 + c
-            gh = psum.tile([P, BB], F32, tag="gh", name="gh")
+            q = c * 3 + g
+            ps = bank([P, BB])
             nc.tensor.matmul_mx(
-                out=gh[:],
+                out=ps[:],
                 lhsT=wc[:, q * P:(q + 1) * P].bitcast(FP8X4),
                 lhsT_scale=wsc[:, q * P:(q + 1) * P],
-                rhs=staged[blk][1][:].bitcast(FP8X4),
-                rhs_scale=staged[blk][2][:],
+                rhs=codes[blk][0][:].bitcast(FP8X4),
+                rhs_scale=codes[blk][1][:],
                 start=True,
                 stop=True,
             )
-            return gh
+            return ps
 
-        def mm_plain(i, g):
-            blk, c = divmod(i, 4)
-            q = g * 4 + c
-            cb = staged[blk][3][:].bitcast(BF16).rearrange("p (b e) -> p b e", e=2)
-            gi = psum.tile([P, BB], F32, tag="gi", name="gi", bufs=2)
-            nc.tensor.matmul(gi[:], lhsT=wiht[:, 0, q, :], rhs=cb[:, :, 0], start=True, stop=False)
-            nc.tensor.matmul(gi[:], lhsT=wiht[:, 1, q, :], rhs=cb[:, :, 1], start=False, stop=(g < 2))
-            if g == 2:
-                nc.tensor.matmul(gi[:], lhsT=xw[:, c, :], rhs=xmv[:, blk * BB:(blk + 1) * BB, 0], start=False, stop=True)
-            return gi
+        def add_t(ps, parts, blk, s):
+            for c in range(4):
+                nc.tensor.matmul(ps[:, c * P:(c + 1) * P], lhsT=parts[blk * 4 + c][:, s * P:(s + 1) * P], rhs=ident_f[:], is_transpose=True, start=False, stop=False)
 
-        def x_term(i, g, t, dst, acc):
-            blk, c = divmod(i, 4)
-            xbv = loaded[blk][2][:].rearrange("p (b i) -> p b i", i=2)
-            nc.vector.scalar_tensor_tensor(out=dst, in0=xbv[:, :, t], scalar=wx[:, g, c // 2, c % 2, t:t + 1], in1=acc, op0=ALU.mult, op1=ALU.add)
+        def sub_mul(k, n, z):
+            blk, s = divmod(k, 4)
+            d = ew.tile([P, H], F32, tag="d", name="d", bufs=5)
+            e1 = nc.vector if k >= NU - 4 else nc.gpsimd
+            e1.tensor_tensor(out=d[:], in0=hs_[blk][:, s, :], in1=n[:], op=ALU.subtract)
+            nc.gpsimd.tensor_tensor(out=d[:], in0=d[:], in1=z[:], op=ALU.mult)
+            return d
 
-        def out_t(k, ps):
-            w, sp = divmod(k, 2)
-            dd, nn = pairs[w]["d"], pairs[w]["n"]
-            for s2 in range(2):
-                for e in range(2):
-                    lo = (2 * sp + s2) * P
-                    nc.tensor.matmul(ps[:, s2, e, :], lhsT=dd[:, e, lo:lo + P], rhs=ident_f[:], is_transpose=True, start=True, stop=False)
-                    nc.tensor.matmul(ps[:, s2, e, :], lhsT=nn[:, e, lo:lo + P], rhs=ident_f[:], is_transpose=True, start=False, stop=True)
+        def add_store(k, n, d):
+            e1 = nc.vector if k >= NU - 4 else nc.gpsimd
+            e1.tensor_tensor(out=d[:], in0=d[:], in1=n[:], op=ALU.add)
+            nc.sync.dma_start(out=out[k * P:(k + 1) * P, :], in_=d[:])
 
-        def out_c(k, ps, on_vector):
-            w, sp = divmod(k, 2)
-            blk, u = divmod(w, 2)
-            if u == 0:
-                obs[(blk, sp)] = outp.tile([P, 2, 512], F32, tag="ob", name="ob")
-            ob = obs[(blk, sp)]
-            dst = ob[:].rearrange("b s (p t) -> b s p t", t=4)[:, :, :, 2 * u:2 * u + 2]
-            src = ps[:].rearrange("b s e p -> b s p e")
-            if on_vector:
-                nc.vector.tensor_copy(out=dst, in_=src)
-            else:
-                nc.scalar.copy(out=dst, in_=src)
-            if u == 1:
-                r0 = blk * BB + sp * 256
-                nc.sync.dma_start(out=out[r0:r0 + 256, :].rearrange("(s b) j -> b s j", b=P), in_=ob[:])
-
-        for j in range(NUNIT + OUT_LAG):
+        for j in range(NU + LAG):
             blk, c = divmod(j, 4)
-            u, e = divmod(c, 2)
-            w = j // 2
-            live = j < NUNIT
-            lag = 1 <= j <= NUNIT
-            jn = j - 1
-            cn = jn % 4
-            wn = jn // 2
+            live = j < NU
+            lag = 1 <= j <= NU
+            k = j - LAG
             nxt = blk + 1
-            k = j - OUT_LAG
+            cols = slice(c * P, (c + 1) * P)
+            if live and c == 0 and blk + 2 < NBLK:
+                load(blk + 2)
             if live:
-                if c == 0 and blk + 2 < NBLK:
-                    load(blk + 2)
-                gi_r = mm_plain(j, 0)
+                gi_r = bank([P, BB])
+                for e in range(2):
+                    nc.tensor.matmul(gi_r[:], lhsT=wt[:, e, 0, cols], rhs=catts[blk][:, e, :], start=(e == 0), stop=(e == 1))
+            if k >= 0:
+                kb, ks = divmod(k, 4)
+                tok = slice(ks * P, (ks + 1) * P)
+                ps_z = bank([P, H])
+                nc.tensor.matmul(ps_z[:], lhsT=catts[kb][:, 0, tok], rhs=wt[:, 0, 1, :], start=True, stop=False)
+                add_t(ps_z, zts, kb, ks)
+            if live and c == 0 and blk > 0:
+                px_t(blk)
+            if k >= 0:
+                nc.tensor.matmul(ps_z[:], lhsT=catts[kb][:, 1, tok], rhs=wt[:, 1, 1, :], start=False, stop=True)
             if lag:
-                gh_n = mm_mx(jn, 2)
+                gh_n = mm_mx(j - 1, 2)
             if live:
-                gi_z = mm_plain(j, 1)
                 gh_r = mm_mx(j, 0)
-            if live:
                 gh_z = mm_mx(j, 1)
-            if lag:
-                gi_n = mm_plain(jn, 2)
-            ps_o = None
-            if 0 <= k:
-                ps_o = psum.tile([P, 2, 2, P], F32, tag="tp", name="ps_o", bufs=2)
-                out_t(k, ps_o)
+            if k >= 0:
+                ps_n = bank([P, H])
+                nc.tensor.matmul(ps_n[:], lhsT=xt[:, k * P:(k + 1) * P], rhs=xw[:], start=True, stop=False)
+                nc.tensor.matmul(ps_n[:], lhsT=catts[kb][:, 0, tok], rhs=wt[:, 0, 2, :], start=False, stop=False)
+                add_t(ps_n, vs, kb, ks)
             ps_i = None
             if live and nxt < NBLK and c < 3:
-                ps_i = psum.tile([P, 2, 2, P], F32, tag="tp", name="ps_i", bufs=2)
-                if c < 2:
-                    stage_h_t(nxt, c, ps_i)
-                else:
-                    stage_cat_t(nxt, ps_i)
+                ps_i = cat_t(nxt) if c == 2 else h_t(nxt, c)
+            if k >= 0:
+                nc.tensor.matmul(ps_n[:], lhsT=catts[kb][:, 1, tok], rhs=wt[:, 1, 2, :], start=False, stop=True)
+            if j < 2:
+                banks = whh_t(j + 2)
+            if j == 3:
+                pw1 = wih_t(1)
+                pw2 = wih_t(2)
+                pz = bank([P, H], BF16)
+                for cc in range(4):
+                    nc.tensor.transpose(pz[:, cc * P:(cc + 1) * P], wih_sb[:, 1, cc, 257:258].to_broadcast([P, P]), ident_b[:])
+            if j == 4:
+                pxw = bank([P, 4, P], BF16)
+                for cc in range(4):
+                    nc.tensor.transpose(pxw[:, cc, :], t4[:, cc, :], ident_b[:])
             if live:
-                if e == 0:
-                    pairs[w] = {
-                        "a1": ew.tile([P, 2, BB], F32, tag="az1", name="az1"),
-                        "a2": ew.tile([P, 2, BB], F32, tag="az2", name="az2"),
-                        "n": ew.tile([P, 2, BB], F32, tag="n", name="n", bufs=3),
-                    }
-                pw = pairs[w]
-                a1 = ew.tile([P, BB], F32, tag="a1", name="a1")
-                x_term(j, 0, 0, a1[:], gi_r[:])
+                xb0 = xbs[blk][:, :, 0]
+                t = ew.tile([P, BB], F32, tag="t", name="t")
+                nc.scalar.activation(out=t[:], in_=xb0, func=ACT.Identity, scale=wz0[:, c:c + 1])
+                a = ew.tile([P, BB], F32, tag="a", name="a")
+                nc.vector.scalar_tensor_tensor(out=a[:], in0=xb0, scalar=wih_sb[:, 0, c, 256:257], in1=gi_r[:], op0=ALU.mult, op1=ALU.add)
+            if k >= 0:
+                az = ew.tile([P, H], F32, tag="az", name="az")
+                nc.vector.scalar_tensor_tensor(out=az[:], in0=wz1[:], scalar=xs[:, k, 1:2], in1=ps_z[:], op0=ALU.mult, op1=ALU.add)
+                z = ew.tile([P, H], F32, tag="z", name="z")
+                nc.scalar.activation(out=z[:], in_=az[:], func=ACT.Sigmoid)
+            if live:
+                nc.vector.scalar_tensor_tensor(out=a[:], in0=pxs[blk][:], scalar=wih_sb[:, 0, c, 257:258], in1=a[:], op0=ALU.mult, op1=ALU.add)
             if lag:
-                v = ew.tile([P, BB], F32, tag="v", name="v")
-                nc.vector.scalar_tensor_tensor(out=v[:], in0=gh_n[:], scalar=bias[:, 20 + cn:21 + cn], in1=units[jn][:], op0=ALU.add, op1=ALU.mult)
+                cn = (j - 1) % 4
+                v = ew.tile([P, BB], F32, tag="v", name="v", bufs=10)
+                nc.vector.scalar_tensor_tensor(out=v[:], in0=gh_n[:], scalar=bias[:, 20 + cn:21 + cn], in1=rs[j - 1][:], op0=ALU.add, op1=ALU.mult)
+                vs[j - 1] = v
             if live:
-                nc.vector.scalar_tensor_tensor(out=a1[:], in0=staged[blk][4][:], scalar=wx[:, 0, u, e, 1:2], in1=a1[:], op0=ALU.mult, op1=ALU.add)
-                x_term(j, 1, 0, pw["a1"][:, e, :], gi_z[:])
-                nc.vector.tensor_tensor(out=a1[:], in0=gh_r[:], in1=a1[:], op=ALU.add)
+                nc.vector.tensor_tensor(out=a[:], in0=gh_r[:], in1=a[:], op=ALU.add)
                 r = ew.tile([P, BB], F32, tag="r", name="r")
-                nc.scalar.activation(out=r[:], in_=a1[:], func=ACT.Sigmoid, bias=brz[:, c:c + 1], scale=1.0)
-                units[j] = r
-            if lag:
-                pn = pairs[wn]
-                nc.vector.tensor_tensor(out=v[:], in0=gi_n[:], in1=v[:], op=ALU.add)
-                nc.scalar.activation(out=pn["n"][:, cn % 2, :], in_=v[:], func=ACT.Tanh, bias=bias[:, 8 + cn:9 + cn], scale=1.0)
-                if cn % 2 == 1:
-                    pn["d"] = ew.tile([P, 2, BB], F32, tag="d", name="d", bufs=3)
-                    un = cn // 2
-                    ht = staged[jn // 4][0][:].rearrange("p (b t) -> p t b", t=4)[:, 2 * un:2 * un + 2, :]
-                    eng = nc.vector if wn == NPAIR - 1 else nc.gpsimd
-                    eng.tensor_tensor(out=pn["d"][:], in0=ht, in1=pn["n"][:], op=ALU.subtract)
-            if live:
-                x_term(j, 1, 1, pw["a2"][:, e, :], gh_z[:])
-                if e == 1:
-                    nc.gpsimd.tensor_tensor(out=pw["a1"][:], in0=pw["a1"][:], in1=pw["a2"][:], op=ALU.add)
-            if j % 2 == 0 and 2 <= j <= NUNIT:
-                wp = w - 1
-                pp = pairs[wp]
-                up = wp % 2
-                z = ew.tile([P, 2, BB], F32, tag="z", name="z")
-                for ez in range(2):
-                    cz = 4 + 2 * up + ez
-                    nc.scalar.activation(out=z[:, ez, :], in_=pp["a1"][:, ez, :], func=ACT.Sigmoid, bias=brz[:, cz:cz + 1], scale=1.0)
-                eng = nc.vector if wp == NPAIR - 1 else nc.gpsimd
-                eng.tensor_tensor(out=pp["d"][:], in0=pp["d"][:], in1=z[:], op=ALU.mult)
-            if ps_o is not None:
-                out_c(k, ps_o, (not live) and k % 2 == 1)
+                nc.scalar.activation(out=r[:], in_=a[:], func=ACT.Sigmoid, bias=brz[:, c:c + 1], scale=1.0)
+                rs[j] = r
+                zt = ew.tile([P, BB], F32, tag="zt", name="zt", bufs=10)
+                nc.vector.scalar_tensor_tensor(out=zt[:], in0=gh_z[:], scalar=brz[:, 4 + c:5 + c], in1=t[:], op0=ALU.add, op1=ALU.add)
+                zts[j] = zt
+            if k >= 0:
+                n = ew.tile([P, H], F32, tag="n", name="n", bufs=4)
+                nc.scalar.activation(out=n[:], in_=ps_n[:], func=ACT.Tanh)
             if ps_i is not None:
-                if c < 2:
-                    stage_h_c(nxt, c, ps_i)
+                if c == 2:
+                    cat_c(nxt, ps_i)
                 else:
-                    stage_cat_c(nxt, ps_i)
-            if live:
-                if c == 2 and nxt < NBLK:
-                    stage_q(nxt)
-                if c == 3 and nxt < NBLK:
-                    x1_bank(nxt)
+                    h_c(nxt, c, ps_i)
+            if live and c == 2 and nxt < NBLK:
+                h_q(nxt)
+            if j < 2:
+                grps[j + 2] = whh_c(j + 2, banks, (nc.scalar, nc.scalar))
+            if j < 3:
+                whh_q(j + 1, grps[j + 1])
+            if j == 3:
+                wih_c(1, pw1, True)
+                wih_c(2, pw2, True)
+                nc.scalar.copy(out=wz1[:], in_=pz[:])
+                nc.vector.tensor_copy(out=t4[:, :, 0:2], in_=wih_sb[:, 2, :, 256:258])
+                nc.vector.tensor_copy(out=t4[:, :, 2], in_=bias[:, 8:12])
+            if j == 4:
+                nc.scalar.copy(out=xw[:], in_=pxw[:].rearrange("p c m -> p (c m)"))
+            if k >= 0:
+                d = sub_mul(k, n, z)
+                if k < NU - 4:
+                    add_store(k, n, d)
+                else:
+                    late.append((k, n, d))
+                    if k > NU - 4:
+                        add_store(*late[-2])
+        add_store(*late[-1])

@@ -235,18 +235,20 @@ def tile_wavernncell_pa_t_kernel(tc, x, feat, aux1, h, w_ih, w_hh, b_ih, b_hh, o
             for c in range(4):
                 nc.tensor.matmul(ps[:, c * P:(c + 1) * P], lhsT=parts[blk * 4 + c][:, s * P:(s + 1) * P], rhs=ident_f[:], is_transpose=True, start=False, stop=False)
 
-        def sub_mul(k, n, z):
+        def sub_mul(k, w, n, z):
             blk, s = divmod(k, 4)
-            d = ew.tile([P, H], F32, tag="d", name="d", bufs=5)
-            e1 = nc.vector if k >= NU - 4 else nc.gpsimd
-            e1.tensor_tensor(out=d[:], in0=hs_[blk][:, s, :], in1=n[:], op=ALU.subtract)
-            nc.gpsimd.tensor_tensor(out=d[:], in0=d[:], in1=z[:], op=ALU.mult)
+            d = ew.tile([P, 2, H], F32, tag="d", name="d", bufs=4)
+            e1 = nc.vector if w == 1 else nc.gpsimd
+            i = k % 2
+            e1.tensor_tensor(out=d[:, i:i + w, :], in0=hs_[blk][:, s:s + w, :], in1=n[:, i:i + w, :], op=ALU.subtract)
+            nc.gpsimd.tensor_tensor(out=d[:, i:i + w, :], in0=d[:, i:i + w, :], in1=z[:, i:i + w, :], op=ALU.mult)
             return d
 
-        def add_store(k, n, d):
-            e1 = nc.vector if k >= NU - 4 else nc.gpsimd
-            e1.tensor_tensor(out=d[:], in0=d[:], in1=n[:], op=ALU.add)
-            nc.sync.dma_start(out=out[k * P:(k + 1) * P, :], in_=d[:])
+        def add_store(k, w, n, d):
+            e1 = nc.vector if w == 1 else nc.gpsimd
+            i = k % 2
+            e1.tensor_tensor(out=d[:, i:i + w, :], in0=d[:, i:i + w, :], in1=n[:, i:i + w, :], op=ALU.add)
+            nc.sync.dma_start(out=out[k * P:(k + w) * P, :].rearrange("(s p) k -> p s k", p=P), in_=d[:, i:i + w, :])
 
         for j in range(NU + LAG):
             blk, c = divmod(j, 4)
@@ -307,8 +309,9 @@ def tile_wavernncell_pa_t_kernel(tc, x, feat, aux1, h, w_ih, w_hh, b_ih, b_hh, o
             if k >= 0:
                 az = ew.tile([P, H], F32, tag="az", name="az")
                 nc.vector.scalar_tensor_tensor(out=az[:], in0=wz1[:], scalar=xs[:, k, 1:2], in1=ps_z[:], op0=ALU.mult, op1=ALU.add)
-                z = ew.tile([P, H], F32, tag="z", name="z")
-                nc.scalar.activation(out=z[:], in_=az[:], func=ACT.Sigmoid)
+                if k % 2 == 0:
+                    z = ew.tile([P, 2, H], F32, tag="z", name="z")
+                nc.scalar.activation(out=z[:, k % 2, :], in_=az[:], func=ACT.Sigmoid)
             if live:
                 nc.vector.scalar_tensor_tensor(out=a[:], in0=pxs[blk][:], scalar=wih_sb[:, 0, c, 257:258], in1=a[:], op0=ALU.mult, op1=ALU.add)
             if lag:
@@ -325,8 +328,9 @@ def tile_wavernncell_pa_t_kernel(tc, x, feat, aux1, h, w_ih, w_hh, b_ih, b_hh, o
                 nc.vector.scalar_tensor_tensor(out=zt[:], in0=gh_z[:], scalar=brz[:, 4 + c:5 + c], in1=t[:], op0=ALU.add, op1=ALU.add)
                 zts[j] = zt
             if k >= 0:
-                n = ew.tile([P, H], F32, tag="n", name="n", bufs=4)
-                nc.scalar.activation(out=n[:], in_=ps_n[:], func=ACT.Tanh)
+                if k % 2 == 0:
+                    n = ew.tile([P, 2, H], F32, tag="n", name="n", bufs=4)
+                nc.scalar.activation(out=n[:, k % 2, :], in_=ps_n[:], func=ACT.Tanh)
             if ps_i is not None:
                 if c == 2:
                     cat_c(nxt, ps_i)
@@ -347,11 +351,13 @@ def tile_wavernncell_pa_t_kernel(tc, x, feat, aux1, h, w_ih, w_hh, b_ih, b_hh, o
             if j == 4:
                 nc.scalar.copy(out=xw[:], in_=pxw[:].rearrange("p c m -> p (c m)"))
             if k >= 0:
-                d = sub_mul(k, n, z)
                 if k < NU - 4:
-                    add_store(k, n, d)
+                    if k % 2 == 1:
+                        d = sub_mul(k - 1, 2, n, z)
+                        add_store(k - 1, 2, n, d)
                 else:
-                    late.append((k, n, d))
+                    d = sub_mul(k, 1, n, z)
+                    late.append((k, 1, n, d))
                     if k > NU - 4:
                         add_store(*late[-2])
         add_store(*late[-1])

@@ -202,13 +202,13 @@ def tile_wavernncell_pa_t_kernel(tc, x, feat, aux1, h, w_ih, w_hh, b_ih, b_hh, o
         psb = bank([P, P], BF16)
         nc.tensor.transpose(psb[:], brow[:], ident_b[:])
         h_q(0)
-        wih_c(0, pw, False)
         nc.vector.tensor_copy(out=xs[:], in_=psx[:, 0:32].bitcast(BF16).rearrange("p (t i) -> p t i", i=2))
+        wih_c(0, pw, False)
         nc.vector.tensor_copy(out=bias[:], in_=psb[:, 0:24])
         nc.vector.tensor_tensor(out=brz[:], in0=bias[:, 0:8], in1=bias[:, 12:20], op=ALU.add)
         nc.vector.tensor_copy(out=wz0[:], in_=wih_sb[:, 1, :, 256:257].rearrange("p c i -> p (c i)"))
-        px_t(0)
         banks = whh_t(1)
+        px_t(0)
         grps = {1: whh_c(1, banks, (nc.scalar, nc.scalar))}
 
         rs = {}
@@ -241,7 +241,7 @@ def tile_wavernncell_pa_t_kernel(tc, x, feat, aux1, h, w_ih, w_hh, b_ih, b_hh, o
             e1 = nc.vector if w == 1 else nc.gpsimd
             i = k % 2
             e1.tensor_tensor(out=d[:, i:i + w, :], in0=hs_[blk][:, s:s + w, :], in1=n[:, i:i + w, :], op=ALU.subtract)
-            nc.gpsimd.tensor_tensor(out=d[:, i:i + w, :], in0=d[:, i:i + w, :], in1=z[:, i:i + w, :], op=ALU.mult)
+            e1.tensor_tensor(out=d[:, i:i + w, :], in0=d[:, i:i + w, :], in1=z[:, i:i + w, :], op=ALU.mult)
             return d
 
         def add_store(k, w, n, d):
@@ -268,26 +268,24 @@ def tile_wavernncell_pa_t_kernel(tc, x, feat, aux1, h, w_ih, w_hh, b_ih, b_hh, o
                 tok = slice(ks * P, (ks + 1) * P)
                 ps_z = bank([P, H])
                 nc.tensor.matmul(ps_z[:], lhsT=catts[kb][:, 0, tok], rhs=wt[:, 0, 1, :], start=True, stop=False)
+                ps_n = bank([P, H])
+                nc.tensor.matmul(ps_n[:], lhsT=xt[:, k * P:(k + 1) * P], rhs=xw[:], start=True, stop=False)
+                nc.tensor.matmul(ps_n[:], lhsT=catts[kb][:, 0, tok], rhs=wt[:, 0, 2, :], start=False, stop=False)
                 add_t(ps_z, zts, kb, ks)
+                add_t(ps_n, vs, kb, ks)
+            ps_i = None
+            if live and nxt < NBLK and c < 3:
+                ps_i = cat_t(nxt) if c == 2 else h_t(nxt, c)
             if live and c == 0 and blk > 0:
                 px_t(blk)
             if k >= 0:
                 nc.tensor.matmul(ps_z[:], lhsT=catts[kb][:, 1, tok], rhs=wt[:, 1, 1, :], start=False, stop=True)
+                nc.tensor.matmul(ps_n[:], lhsT=catts[kb][:, 1, tok], rhs=wt[:, 1, 2, :], start=False, stop=True)
             if lag:
                 gh_n = mm_mx(j - 1, 2)
             if live:
                 gh_r = mm_mx(j, 0)
                 gh_z = mm_mx(j, 1)
-            if k >= 0:
-                ps_n = bank([P, H])
-                nc.tensor.matmul(ps_n[:], lhsT=xt[:, k * P:(k + 1) * P], rhs=xw[:], start=True, stop=False)
-                nc.tensor.matmul(ps_n[:], lhsT=catts[kb][:, 0, tok], rhs=wt[:, 0, 2, :], start=False, stop=False)
-                add_t(ps_n, vs, kb, ks)
-            ps_i = None
-            if live and nxt < NBLK and c < 3:
-                ps_i = cat_t(nxt) if c == 2 else h_t(nxt, c)
-            if k >= 0:
-                nc.tensor.matmul(ps_n[:], lhsT=catts[kb][:, 1, tok], rhs=wt[:, 1, 2, :], start=False, stop=True)
             if j < 2:
                 banks = whh_t(j + 2)
             if j == 3:
@@ -309,6 +307,9 @@ def tile_wavernncell_pa_t_kernel(tc, x, feat, aux1, h, w_ih, w_hh, b_ih, b_hh, o
             if k >= 0:
                 az = ew.tile([P, H], F32, tag="az", name="az")
                 nc.vector.scalar_tensor_tensor(out=az[:], in0=wz1[:], scalar=xs[:, k, 1:2], in1=ps_z[:], op0=ALU.mult, op1=ALU.add)
+                if k > NU - 4:
+                    kl, nl, zl = late[-1]
+                    add_store(kl, 1, nl, sub_mul(kl, 1, nl, zl))
                 if k % 2 == 0:
                     z = ew.tile([P, 2, H], F32, tag="z", name="z")
                 nc.scalar.activation(out=z[:, k % 2, :], in_=az[:], func=ACT.Sigmoid)
@@ -356,8 +357,6 @@ def tile_wavernncell_pa_t_kernel(tc, x, feat, aux1, h, w_ih, w_hh, b_ih, b_hh, o
                         d = sub_mul(k - 1, 2, n, z)
                         add_store(k - 1, 2, n, d)
                 else:
-                    d = sub_mul(k, 1, n, z)
-                    late.append((k, 1, n, d))
-                    if k > NU - 4:
-                        add_store(*late[-2])
-        add_store(*late[-1])
+                    late.append((k, n, z))
+        k, n, z = late[-1]
+        add_store(k, 1, n, sub_mul(k, 1, n, z))

@@ -30,7 +30,7 @@ def tile_wavernncell_pa_t_kernel(tc, x, feat, aux1, h, w_ih, w_hh, b_ih, b_hh, o
         ld = ctx.enter_context(tc.tile_pool(name="ld", bufs=3))
         stage = ctx.enter_context(tc.tile_pool(name="stage", bufs=3))
         ew = ctx.enter_context(tc.tile_pool(name="ew", bufs=3))
-        psum = ctx.enter_context(tc.psum_pool(name="psum", bufs=7))
+        psum = ctx.enter_context(tc.psum_pool(name="psum", bufs=1))
         ctx.enter_context(tc.manual_schedule())
 
         xf = x.rearrange("b i -> (b i)")
@@ -76,8 +76,8 @@ def tile_wavernncell_pa_t_kernel(tc, x, feat, aux1, h, w_ih, w_hh, b_ih, b_hh, o
         catts = {}
         pxs = {}
 
-        def bank(shape, dtype=F32):
-            return psum.tile(shape, dtype, tag="ring", name="ring", bufs=7)
+        def bank(tag, shape, dtype=F32):
+            return psum.tile(shape, dtype, tag=tag, name=tag, bufs=(3 if tag == "gh" else 1))
 
         def load(blk):
             hs_[blk] = ld.tile([P, 4, H], BF16, tag="h", name="h_sb", bufs=5)
@@ -88,8 +88,8 @@ def tile_wavernncell_pa_t_kernel(tc, x, feat, aux1, h, w_ih, w_hh, b_ih, b_hh, o
             xbs[blk] = ld.tile([P, BB, 2], BF16, tag="xb", name="xb")
             nc.sync.dma_start(out=xbs[blk][:].rearrange("p b i -> p (b i)"), in_=xf[blk * 2 * BB:(blk + 1) * 2 * BB].partition_broadcast(P))
 
-        def h_t(blk, half):
-            ps = bank([P, 2, 2, P])
+        def h_t(blk, half, tag="tp"):
+            ps = bank(tag, [P, 2, 2, P])
             hw = hs_[blk][:].bitcast(F32)
             for s2 in range(2):
                 for uu in range(2):
@@ -108,8 +108,8 @@ def tile_wavernncell_pa_t_kernel(tc, x, feat, aux1, h, w_ih, w_hh, b_ih, b_hh, o
             nc.vector.quantize_mx(out=hc[:].bitcast(FP8X4), scales=hsc[:], in_=hgrps[blk][:])
             codes[blk] = (hc, hsc)
 
-        def cat_t(blk):
-            ps = bank([P, 4, P])
+        def cat_t(blk, tag="tp"):
+            ps = bank(tag, [P, 4, P])
             cw = cats[blk][:].bitcast(F32)
             for s in range(4):
                 nc.tensor.transpose(ps[:, s, :], cw[:, s, :], ident_f[:])
@@ -120,15 +120,15 @@ def tile_wavernncell_pa_t_kernel(tc, x, feat, aux1, h, w_ih, w_hh, b_ih, b_hh, o
             nc.scalar.copy(out=catts[blk][:], in_=ps[:].rearrange("w s b -> w (s b)").bitcast(BF16).rearrange("w (b e) -> w e b", e=2))
 
         def px_t(blk):
-            px = psum.tile([P, BB], BF16, tag="px", name="px", bufs=1)
+            px = bank("px", [P, BB], BF16)
             for s in range(4):
                 nc.tensor.transpose(px[:, s * P:(s + 1) * P], xs[:, blk * 4 + s, 1:2].to_broadcast([P, P]), ident_b[:])
             pxs[blk] = px
 
         def whh_t(c):
             banks = []
-            for gs in ((0, 1), (2,)):
-                ps = bank([P, len(gs), 2, P])
+            for tag, gs in (("z", (0, 1)), ("n", (2,))):
+                ps = bank(tag, [P, len(gs), 2, P])
                 for j, g in enumerate(gs):
                     for uu in range(2):
                         nc.tensor.transpose(ps[:, j, uu, :], whh_w[:, c, g, uu:256:2], ident_f[:])
@@ -153,8 +153,8 @@ def tile_wavernncell_pa_t_kernel(tc, x, feat, aux1, h, w_ih, w_hh, b_ih, b_hh, o
                 a, b = (c * 3 + lo) * P, (c * 3 + lo + n) * P
                 nc.vector.quantize_mx(out=wc[:, a:b].bitcast(FP8X4), scales=wsc[:, a:b], in_=grp[:, lo * H:(lo + n) * H])
 
-        def wih_t(g):
-            ps = bank([P, 4, P])
+        def wih_t(g, tag):
+            ps = bank(tag, [P, 4, P])
             for c in range(4):
                 nc.tensor.transpose(ps[:, c, :], wih_w[:, g, c, 0:P], ident_f[:])
             return ps
@@ -190,16 +190,16 @@ def tile_wavernncell_pa_t_kernel(tc, x, feat, aux1, h, w_ih, w_hh, b_ih, b_hh, o
         banks = whh_t(0)
         grp = whh_c(0, banks, (nc.vector, nc.scalar))
         ph0 = h_t(0, 0)
-        ph1 = h_t(0, 1)
+        ph1 = h_t(0, 1, "gi")
         h_c(0, 0, ph0)
         h_c(0, 1, ph1)
         whh_q(0, grp)
-        pc = cat_t(0)
+        pc = cat_t(0, "gh")
         cat_c(0, pc)
-        pw = wih_t(0)
-        psx = bank([P, P])
+        pw = wih_t(0, "gh")
+        psx = bank("gh", [P, P])
         nc.tensor.transpose(psx[:], xrow[:].bitcast(F32), ident_f[:])
-        psb = bank([P, P], BF16)
+        psb = bank("px", [P, P], BF16)
         nc.tensor.transpose(psb[:], brow[:], ident_b[:])
         h_q(0)
         nc.vector.tensor_copy(out=xs[:], in_=psx[:, 0:32].bitcast(BF16).rearrange("p (t i) -> p t i", i=2))
@@ -212,14 +212,18 @@ def tile_wavernncell_pa_t_kernel(tc, x, feat, aux1, h, w_ih, w_hh, b_ih, b_hh, o
         grps = {1: whh_c(1, banks, (nc.scalar, nc.scalar))}
 
         rs = {}
-        late = []
         zts = {}
         vs = {}
+        gis = {}
+        acc = {}
+        ts = {}
+        opened = {}
+        late = []
 
         def mm_mx(i, g):
             blk, c = divmod(i, 4)
             q = c * 3 + g
-            ps = bank([P, BB])
+            ps = bank("gh", [P, BB])
             nc.tensor.matmul_mx(
                 out=ps[:],
                 lhsT=wc[:, q * P:(q + 1) * P].bitcast(FP8X4),
@@ -231,24 +235,61 @@ def tile_wavernncell_pa_t_kernel(tc, x, feat, aux1, h, w_ih, w_hh, b_ih, b_hh, o
             )
             return ps
 
-        def add_t(ps, parts, blk, s):
-            for c in range(4):
-                nc.tensor.matmul(ps[:, c * P:(c + 1) * P], lhsT=parts[blk * 4 + c][:, s * P:(s + 1) * P], rhs=ident_f[:], is_transpose=True, start=False, stop=False)
+        def mm_gi(i):
+            blk, c = divmod(i, 4)
+            ps = bank("gi", [P, BB])
+            for e in range(2):
+                nc.tensor.matmul(ps[:], lhsT=wt[:, e, 0, c * P:(c + 1) * P], rhs=catts[blk][:, e, :], start=(e == 0), stop=(e == 1))
+            gis[i] = ps
 
-        def sub_mul(k, w, n, z):
+        def r1(i):
+            blk, c = divmod(i, 4)
+            acc[i] = ew.tile([P, BB], F32, tag="a", name="a")
+            nc.vector.scalar_tensor_tensor(out=acc[i][:], in0=xbs[blk][:, :, 0], scalar=wih_sb[:, 0, c, 256:257], in1=gis[i][:], op0=ALU.mult, op1=ALU.add)
+
+        def r2(i):
+            blk, c = divmod(i, 4)
+            nc.vector.scalar_tensor_tensor(out=acc[i][:], in0=pxs[blk][:], scalar=wih_sb[:, 0, c, 257:258], in1=acc[i][:], op0=ALU.mult, op1=ALU.add)
+
+        def z_term(i):
+            blk, c = divmod(i, 4)
+            ts[i] = ew.tile([P, BB], F32, tag="t", name="t")
+            nc.scalar.activation(out=ts[i][:], in_=xbs[blk][:, :, 0], func=ACT.Identity, scale=wz0[:, c:c + 1])
+
+        def open_sums(k):
+            kb, ks = divmod(k, 4)
+            tok = slice(ks * P, (ks + 1) * P)
+            ps_z = bank("z", [P, H])
+            nc.tensor.matmul(ps_z[:], lhsT=catts[kb][:, 0, tok], rhs=wt[:, 0, 1, :], start=True, stop=False)
+            ps_n = bank("n", [P, H])
+            nc.tensor.matmul(ps_n[:], lhsT=xt[:, k * P:(k + 1) * P], rhs=xw[:], start=True, stop=False)
+            nc.tensor.matmul(ps_n[:], lhsT=catts[kb][:, 0, tok], rhs=wt[:, 0, 2, :], start=False, stop=False)
+            for ps, parts in ((ps_z, zts), (ps_n, vs)):
+                for c in range(4):
+                    nc.tensor.matmul(ps[:, c * P:(c + 1) * P], lhsT=parts[kb * 4 + c][:, tok], rhs=ident_f[:], is_transpose=True, start=False, stop=False)
+            opened[k] = (ps_z, ps_n)
+
+        def close_sums(k):
+            kb, ks = divmod(k, 4)
+            tok = slice(ks * P, (ks + 1) * P)
+            for g, ps in enumerate(opened[k]):
+                nc.tensor.matmul(ps[:], lhsT=catts[kb][:, 1, tok], rhs=wt[:, 1, 1 + g, :], start=False, stop=True)
+
+        def blend(k, w, n, z):
             blk, s = divmod(k, 4)
-            d = ew.tile([P, 2, H], F32, tag="d", name="d", bufs=4)
-            e1 = nc.vector if w == 1 else nc.gpsimd
+            d = ew.tile([P, 2, H], F32, tag="d", name="d", bufs=6)
+            eng = nc.vector if w == 1 else nc.gpsimd
             i = k % 2
-            e1.tensor_tensor(out=d[:, i:i + w, :], in0=hs_[blk][:, s:s + w, :], in1=n[:, i:i + w, :], op=ALU.subtract)
-            e1.tensor_tensor(out=d[:, i:i + w, :], in0=d[:, i:i + w, :], in1=z[:, i:i + w, :], op=ALU.mult)
-            return d
+            dd, nn, zz = (t[:, i:i + w, :] for t in (d, n, z))
+            eng.tensor_tensor(out=dd, in0=hs_[blk][:, s:s + w, :], in1=nn, op=ALU.subtract)
+            eng.tensor_tensor(out=dd, in0=dd, in1=zz, op=ALU.mult)
+            eng.tensor_tensor(out=dd, in0=dd, in1=nn, op=ALU.add)
+            nc.sync.dma_start(out=out[k * P:(k + w) * P, :].rearrange("(s p) k -> p s k", p=P), in_=dd)
 
-        def add_store(k, w, n, d):
-            e1 = nc.vector if w == 1 else nc.gpsimd
-            i = k % 2
-            e1.tensor_tensor(out=d[:, i:i + w, :], in0=d[:, i:i + w, :], in1=n[:, i:i + w, :], op=ALU.add)
-            nc.sync.dma_start(out=out[k * P:(k + w) * P, :].rearrange("(s p) k -> p s k", p=P), in_=d[:, i:i + w, :])
+        mm_gi(0)
+        r1(0)
+        z_term(0)
+        r2(0)
 
         for j in range(NU + LAG):
             blk, c = divmod(j, 4)
@@ -256,82 +297,70 @@ def tile_wavernncell_pa_t_kernel(tc, x, feat, aux1, h, w_ih, w_hh, b_ih, b_hh, o
             lag = 1 <= j <= NU
             k = j - LAG
             nxt = blk + 1
-            cols = slice(c * P, (c + 1) * P)
             if live and c == 0 and blk + 2 < NBLK:
                 load(blk + 2)
-            if live:
-                gi_r = bank([P, BB])
-                for e in range(2):
-                    nc.tensor.matmul(gi_r[:], lhsT=wt[:, e, 0, cols], rhs=catts[blk][:, e, :], start=(e == 0), stop=(e == 1))
             if k >= 0:
-                kb, ks = divmod(k, 4)
-                tok = slice(ks * P, (ks + 1) * P)
-                ps_z = bank([P, H])
-                nc.tensor.matmul(ps_z[:], lhsT=catts[kb][:, 0, tok], rhs=wt[:, 0, 1, :], start=True, stop=False)
-                ps_n = bank([P, H])
-                nc.tensor.matmul(ps_n[:], lhsT=xt[:, k * P:(k + 1) * P], rhs=xw[:], start=True, stop=False)
-                nc.tensor.matmul(ps_n[:], lhsT=catts[kb][:, 0, tok], rhs=wt[:, 0, 2, :], start=False, stop=False)
-                add_t(ps_z, zts, kb, ks)
-                add_t(ps_n, vs, kb, ks)
-            ps_i = None
-            if live and nxt < NBLK and c < 3:
-                ps_i = cat_t(nxt) if c == 2 else h_t(nxt, c)
-            if live and c == 0 and blk > 0:
-                px_t(blk)
-            if k >= 0:
-                nc.tensor.matmul(ps_z[:], lhsT=catts[kb][:, 1, tok], rhs=wt[:, 1, 1, :], start=False, stop=True)
-                nc.tensor.matmul(ps_n[:], lhsT=catts[kb][:, 1, tok], rhs=wt[:, 1, 2, :], start=False, stop=True)
+                close_sums(k)
             if lag:
                 gh_n = mm_mx(j - 1, 2)
             if live:
                 gh_r = mm_mx(j, 0)
                 gh_z = mm_mx(j, 1)
-            if j < 2:
-                banks = whh_t(j + 2)
-            if j == 3:
-                pw1 = wih_t(1)
-                pw2 = wih_t(2)
-                pz = bank([P, H], BF16)
-                for cc in range(4):
-                    nc.tensor.transpose(pz[:, cc * P:(cc + 1) * P], wih_sb[:, 1, cc, 257:258].to_broadcast([P, P]), ident_b[:])
-            if j == 4:
-                pxw = bank([P, 4, P], BF16)
-                for cc in range(4):
-                    nc.tensor.transpose(pxw[:, cc, :], t4[:, cc, :], ident_b[:])
-            if live:
-                xb0 = xbs[blk][:, :, 0]
-                t = ew.tile([P, BB], F32, tag="t", name="t")
-                nc.scalar.activation(out=t[:], in_=xb0, func=ACT.Identity, scale=wz0[:, c:c + 1])
-                a = ew.tile([P, BB], F32, tag="a", name="a")
-                nc.vector.scalar_tensor_tensor(out=a[:], in0=xb0, scalar=wih_sb[:, 0, c, 256:257], in1=gi_r[:], op0=ALU.mult, op1=ALU.add)
+            if j + 1 < NU:
+                mm_gi(j + 1)
+            if j < 3:
+                whh_q(j + 1, grps[j + 1])
             if k >= 0:
-                az = ew.tile([P, H], F32, tag="az", name="az")
-                nc.vector.scalar_tensor_tensor(out=az[:], in0=wz1[:], scalar=xs[:, k, 1:2], in1=ps_z[:], op0=ALU.mult, op1=ALU.add)
-                if k > NU - 4:
-                    kl, nl, zl = late[-1]
-                    add_store(kl, 1, nl, sub_mul(kl, 1, nl, zl))
                 if k % 2 == 0:
+                    n = ew.tile([P, 2, H], F32, tag="n", name="n", bufs=4)
                     z = ew.tile([P, 2, H], F32, tag="z", name="z")
-                nc.scalar.activation(out=z[:, k % 2, :], in_=az[:], func=ACT.Sigmoid)
-            if live:
-                nc.vector.scalar_tensor_tensor(out=a[:], in0=pxs[blk][:], scalar=wih_sb[:, 0, c, 257:258], in1=a[:], op0=ALU.mult, op1=ALU.add)
+                nc.scalar.activation(out=n[:, k % 2, :], in_=opened[k][1][:], func=ACT.Tanh)
+                az = ew.tile([P, H], F32, tag="az", name="az")
+                nc.vector.scalar_tensor_tensor(out=az[:], in0=wz1[:], scalar=xs[:, k, 1:2], in1=opened[k][0][:], op0=ALU.mult, op1=ALU.add)
             if lag:
                 cn = (j - 1) % 4
                 v = ew.tile([P, BB], F32, tag="v", name="v", bufs=10)
                 nc.vector.scalar_tensor_tensor(out=v[:], in0=gh_n[:], scalar=bias[:, 20 + cn:21 + cn], in1=rs[j - 1][:], op0=ALU.add, op1=ALU.mult)
                 vs[j - 1] = v
+            if 0 <= k + 1 < NU:
+                open_sums(k + 1)
+            ps_i = None
+            if live and nxt < NBLK:
+                if c < 2:
+                    ps_i = h_t(nxt, c)
+                elif c == 2:
+                    ps_i = cat_t(nxt)
+            if j < 2:
+                banks = whh_t(j + 2)
+            if j == 2:
+                pz = bank("z", [P, H], BF16)
+                pxw = bank("n", [P, 4, P], BF16)
+                for cc in range(4):
+                    nc.tensor.transpose(pz[:, cc * P:(cc + 1) * P], wih_sb[:, 1, cc, 257:258].to_broadcast([P, P]), ident_b[:])
+                    nc.tensor.transpose(pxw[:, cc, :], t4[:, cc, :], ident_b[:])
+            if j == 3:
+                pw1 = wih_t(1, "z")
+                pw2 = wih_t(2, "n")
             if live:
-                nc.vector.tensor_tensor(out=a[:], in0=gh_r[:], in1=a[:], op=ALU.add)
-                r = ew.tile([P, BB], F32, tag="r", name="r")
-                nc.scalar.activation(out=r[:], in_=a[:], func=ACT.Sigmoid, bias=brz[:, c:c + 1], scale=1.0)
-                rs[j] = r
+                nc.vector.tensor_tensor(out=acc[j][:], in0=gh_r[:], in1=acc[j][:], op=ALU.add)
+            if j + 1 < NU:
+                r1(j + 1)
+            if live:
                 zt = ew.tile([P, BB], F32, tag="zt", name="zt", bufs=10)
-                nc.vector.scalar_tensor_tensor(out=zt[:], in0=gh_z[:], scalar=brz[:, 4 + c:5 + c], in1=t[:], op0=ALU.add, op1=ALU.add)
+                nc.vector.scalar_tensor_tensor(out=zt[:], in0=gh_z[:], scalar=brz[:, 4 + c:5 + c], in1=ts[j][:], op0=ALU.add, op1=ALU.add)
                 zts[j] = zt
+            if live and c == 3 and nxt < NBLK:
+                px_t(nxt)
+            if j + 1 < NU:
+                r2(j + 1)
             if k >= 0:
-                if k % 2 == 0:
-                    n = ew.tile([P, 2, H], F32, tag="n", name="n", bufs=4)
-                nc.scalar.activation(out=n[:, k % 2, :], in_=ps_n[:], func=ACT.Tanh)
+                nc.scalar.activation(out=z[:, k % 2, :], in_=az[:], func=ACT.Sigmoid)
+            if live:
+                r = ew.tile([P, BB], F32, tag="r", name="r")
+                nc.scalar.activation(out=r[:], in_=acc[j][:], func=ACT.Sigmoid, bias=brz[:, c:c + 1], scale=1.0)
+                rs[j] = r
+            if j + 1 < NU:
+                z_term(j + 1)
             if ps_i is not None:
                 if c == 2:
                     cat_c(nxt, ps_i)
@@ -339,24 +368,24 @@ def tile_wavernncell_pa_t_kernel(tc, x, feat, aux1, h, w_ih, w_hh, b_ih, b_hh, o
                     h_c(nxt, c, ps_i)
             if live and c == 2 and nxt < NBLK:
                 h_q(nxt)
+            if j == 0:
+                nc.vector.tensor_copy(out=t4[:, :, 0:2], in_=wih_sb[:, 2, :, 256:258])
+                nc.vector.tensor_copy(out=t4[:, :, 2], in_=bias[:, 8:12])
             if j < 2:
                 grps[j + 2] = whh_c(j + 2, banks, (nc.scalar, nc.scalar))
-            if j < 3:
-                whh_q(j + 1, grps[j + 1])
+            if j == 2:
+                nc.scalar.copy(out=wz1[:], in_=pz[:])
+                nc.scalar.copy(out=xw[:], in_=pxw[:].rearrange("p c m -> p (c m)"))
             if j == 3:
                 wih_c(1, pw1, True)
                 wih_c(2, pw2, True)
-                nc.scalar.copy(out=wz1[:], in_=pz[:])
-                nc.vector.tensor_copy(out=t4[:, :, 0:2], in_=wih_sb[:, 2, :, 256:258])
-                nc.vector.tensor_copy(out=t4[:, :, 2], in_=bias[:, 8:12])
-            if j == 4:
-                nc.scalar.copy(out=xw[:], in_=pxw[:].rearrange("p c m -> p (c m)"))
             if k >= 0:
-                if k < NU - 4:
-                    if k % 2 == 1:
-                        d = sub_mul(k - 1, 2, n, z)
-                        add_store(k - 1, 2, n, d)
-                else:
+                if k >= NU - 4:
                     late.append((k, n, z))
-        k, n, z = late[-1]
-        add_store(k, 1, n, sub_mul(k, 1, n, z))
+                    if len(late) > 1:
+                        kl, nl, zl = late[-2]
+                        blend(kl, 1, nl, zl)
+                elif k % 2 == 1:
+                    blend(k - 1, 2, n, z)
+        kl, nl, zl = late[-1]
+        blend(kl, 1, nl, zl)

@@ -16,9 +16,12 @@ B = 4096
 H = 512
 IN = 258
 BB = 512
-NBLK = B // BB
+SIZES = [256] + [BB] * 7 + [256]
+STARTS = [sum(SIZES[:b]) for b in range(len(SIZES))]
+NBLK = len(SIZES)
 NU = NBLK * 4
-LAG = 5
+NSLAB = B // P
+VEC_FROM = NSLAB - 4
 WROW = 264
 FLOPS = 2 * B * 3 * H * (H + IN)
 
@@ -29,7 +32,7 @@ def tile_wavernncell_pa_t_kernel(tc, x, feat, aux1, h, w_ih, w_hh, b_ih, b_hh, o
         const = ctx.enter_context(tc.tile_pool(name="const", bufs=1))
         ld = ctx.enter_context(tc.tile_pool(name="ld", bufs=3))
         stage = ctx.enter_context(tc.tile_pool(name="stage", bufs=3))
-        ew = ctx.enter_context(tc.tile_pool(name="ew", bufs=3))
+        ew = ctx.enter_context(tc.tile_pool(name="ew", bufs=2))
         psum = ctx.enter_context(tc.psum_pool(name="psum", bufs=1))
         ctx.enter_context(tc.manual_schedule())
 
@@ -64,7 +67,7 @@ def tile_wavernncell_pa_t_kernel(tc, x, feat, aux1, h, w_ih, w_hh, b_ih, b_hh, o
         xw = const.tile([P, H], BF16, name="xw")
         bias = const.tile([P, 24], F32, name="bias")
         brz = const.tile([P, 8], F32, name="brz")
-        xs = const.tile([P, B // P, 2], BF16, name="xs")
+        xs = const.tile([P, NSLAB, 2], BF16, name="xs")
         whh_w = whh_sb[:].bitcast(F32)
         wih_w = wih_sb[:].bitcast(F32)
 
@@ -75,55 +78,73 @@ def tile_wavernncell_pa_t_kernel(tc, x, feat, aux1, h, w_ih, w_hh, b_ih, b_hh, o
         codes = {}
         catts = {}
         pxs = {}
+        perms = {}
 
         def bank(tag, shape, dtype=F32):
             return psum.tile(shape, dtype, tag=tag, name=tag, bufs=(3 if tag == "gh" else 1))
 
-        def load(blk):
-            hs_[blk] = ld.tile([P, 4, H], BF16, tag="h", name="h_sb", bufs=5)
-            nc.sync.dma_start(out=hs_[blk][:], in_=h[blk * BB:(blk + 1) * BB, :].rearrange("(s p) k -> p s k", p=P))
-            cats[blk] = ld.tile([P, 4, 256], BF16, tag="cat", name="cat")
-            nc.sync.dma_start(out=cats[blk][:, :, 0:128], in_=feat[blk * BB:(blk + 1) * BB, :].rearrange("(s p) k -> p s k", p=P))
-            nc.sync.dma_start(out=cats[blk][:, :, 128:256], in_=aux1[blk * BB:(blk + 1) * BB, :].rearrange("(s p) k -> p s k", p=P))
-            xbs[blk] = ld.tile([P, BB, 2], BF16, tag="xb", name="xb")
-            nc.sync.dma_start(out=xbs[blk][:].rearrange("p b i -> p (b i)"), in_=xf[blk * 2 * BB:(blk + 1) * 2 * BB].partition_broadcast(P))
+        def load_h(b):
+            t0, n = STARTS[b], SIZES[b]
+            hs_[b] = ld.tile([P, 4, H], BF16, tag="h", name="h_sb", bufs=5)
+            nc.sync.dma_start(out=hs_[b][:, 0:n // P, :], in_=h[t0:t0 + n, :].rearrange("(s p) k -> p s k", p=P))
 
-        def h_t(blk, half, tag="tp"):
+        def load_cat(b):
+            t0, n = STARTS[b], SIZES[b]
+            cats[b] = ld.tile([P, 4, 256], BF16, tag="cat", name="cat")
+            nc.sync.dma_start(out=cats[b][:, 0:n // P, 0:128], in_=feat[t0:t0 + n, :].rearrange("(s p) k -> p s k", p=P))
+            nc.sync.dma_start(out=cats[b][:, 0:n // P, 128:256], in_=aux1[t0:t0 + n, :].rearrange("(s p) k -> p s k", p=P))
+
+        def load_xb(b):
+            t0, n = STARTS[b], SIZES[b]
+            xbs[b] = ld.tile([P, BB, 2], BF16, tag="xb", name="xb")
+            nc.sync.dma_start(out=xbs[b][:, 0:n, :].rearrange("p b i -> p (b i)"), in_=xf[2 * t0:2 * (t0 + n)].partition_broadcast(P))
+
+        def h_p(b, half):
+            hp = stage.tile([P, 2, 2, P], F32, tag="hp", name="hp")
+            hw = hs_[b][:].bitcast(F32)
+            nc.scalar.copy(out=hp[:], in_=hw[:, half * 2:half * 2 + 2, :].rearrange("p s (w u) -> p s u w", u=2))
+            perms[(b, half)] = hp
+
+        def h_t(b, half, tag="tp"):
             ps = bank(tag, [P, 2, 2, P])
-            hw = hs_[blk][:].bitcast(F32)
+            hw = hs_[b][:].bitcast(F32)
             for s2 in range(2):
                 for uu in range(2):
-                    nc.tensor.transpose(ps[:, uu, s2, :], hw[:, half * 2 + s2, uu:256:2], ident_f[:])
+                    src = perms[(b, half)][:, s2, uu, :] if (b, half) in perms else hw[:, half * 2 + s2, uu:256:2]
+                    nc.tensor.transpose(ps[:, uu, s2, :], src, ident_f[:])
             return ps
 
-        def h_c(blk, half, ps):
+        def h_c(b, half, ps):
             if half == 0:
-                hgrps[blk] = stage.tile([P, 4 * BB], BF16, tag="hgrp", name="hgrp", bufs=2, align_bytes=64)
-            dst = hgrps[blk][:].bitcast(F32)[:, half * 512:(half + 1) * 512].rearrange("p (b u) -> p b u", u=2)
+                hgrps[b] = stage.tile([P, 4 * BB], BF16, tag="hgrp", name="hgrp", bufs=2, align_bytes=64)
+            dst = hgrps[b][:].bitcast(F32)[:, half * 512:(half + 1) * 512].rearrange("p (b u) -> p b u", u=2)
             nc.scalar.copy(out=dst, in_=ps[:].rearrange("p u s b -> p (s b) u"))
 
-        def h_q(blk):
+        def h_q(b):
+            n = SIZES[b]
             hc = stage.tile([P, BB], U32, tag="hc", name="hc", align_bytes=64)
             hsc = stage.tile([P, BB], U8, tag="hsc", name="hsc", align_bytes=64)
-            nc.vector.quantize_mx(out=hc[:].bitcast(FP8X4), scales=hsc[:], in_=hgrps[blk][:])
-            codes[blk] = (hc, hsc)
+            nc.vector.quantize_mx(out=hc[:, 0:n].bitcast(FP8X4), scales=hsc[:, 0:n], in_=hgrps[b][:, 0:4 * n])
+            codes[b] = (hc, hsc)
 
-        def cat_t(blk, tag="tp"):
+        def cat_t(b, tag="tp"):
             ps = bank(tag, [P, 4, P])
-            cw = cats[blk][:].bitcast(F32)
-            for s in range(4):
+            cw = cats[b][:].bitcast(F32)
+            for s in range(SIZES[b] // P):
                 nc.tensor.transpose(ps[:, s, :], cw[:, s, :], ident_f[:])
             return ps
 
-        def cat_c(blk, ps):
-            catts[blk] = stage.tile([P, 2, BB], BF16, tag="catt", name="catt")
-            nc.scalar.copy(out=catts[blk][:], in_=ps[:].rearrange("w s b -> w (s b)").bitcast(BF16).rearrange("w (b e) -> w e b", e=2))
+        def cat_c(b, ps):
+            n = SIZES[b]
+            catts[b] = stage.tile([P, 2, BB], BF16, tag="catt", name="catt")
+            src = ps[:].rearrange("w s b -> w (s b)")[:, 0:n].bitcast(BF16).rearrange("w (b e) -> w e b", e=2)
+            nc.scalar.copy(out=catts[b][:, :, 0:n], in_=src)
 
-        def px_t(blk):
+        def px_t(b):
             px = bank("px", [P, BB], BF16)
-            for s in range(4):
-                nc.tensor.transpose(px[:, s * P:(s + 1) * P], xs[:, blk * 4 + s, 1:2].to_broadcast([P, P]), ident_b[:])
-            pxs[blk] = px
+            for s in range(SIZES[b] // P):
+                nc.tensor.transpose(px[:, s * P:(s + 1) * P], xs[:, STARTS[b] // P + s, 1:2].to_broadcast([P, P]), ident_b[:])
+            pxs[b] = px
 
         def whh_t(c):
             banks = []
@@ -166,48 +187,45 @@ def tile_wavernncell_pa_t_kernel(tc, x, feat, aux1, h, w_ih, w_hh, b_ih, b_hh, o
             else:
                 nc.vector.tensor_copy(out=wt[:, :, g, :], in_=src)
 
-        nc.sync.dma_start(out=whh_sb[:, 0, :, :], in_=whh_v[:, :, 0, :])
-        hs_[0] = ld.tile([P, 4, H], BF16, tag="h", name="h_sb", bufs=5)
-        nc.sync.dma_start(out=hs_[0][:], in_=h[0:BB, :].rearrange("(s p) k -> p s k", p=P))
-        cats[0] = ld.tile([P, 4, 256], BF16, tag="cat", name="cat")
-        nc.sync.dma_start(out=cats[0][:, :, 0:128], in_=feat[0:BB, :].rearrange("(s p) k -> p s k", p=P))
-        nc.sync.dma_start(out=cats[0][:, :, 128:256], in_=aux1[0:BB, :].rearrange("(s p) k -> p s k", p=P))
+        load_cat(0)
         nc.sync.dma_start(out=wih_sb[:, 0, :, 0:IN], in_=wih_v[:, 0, :, :])
+        nc.sync.dma_start(out=whh_sb[:, 0, :, :], in_=whh_v[:, :, 0, :])
+        load_h(0)
         nc.scalar.dma_start(out=xrow[0:32, :], in_=xf.rearrange("(t c) -> t c", c=256))
         nc.scalar.dma_start(out=brow[0:12, :], in_=b_ih.rearrange("(r c) -> r c", c=P))
         nc.scalar.dma_start(out=brow[12:24, :], in_=b_hh.rearrange("(r c) -> r c", c=P))
-        xbs[0] = ld.tile([P, BB, 2], BF16, tag="xb", name="xb")
-        nc.sync.dma_start(out=xbs[0][:].rearrange("p b i -> p (b i)"), in_=xf[0:2 * BB].partition_broadcast(P))
+        load_xb(0)
+        nc.sync.dma_start(out=whh_sb[:, 1, :, :], in_=whh_v[:, :, 1, :])
         nc.sync.dma_start(out=wih_sb[:, 1, :, 0:IN], in_=wih_v[:, 1, :, :])
-        for c in range(1, 4):
-            nc.sync.dma_start(out=whh_sb[:, c, :, :], in_=whh_v[:, :, c, :])
+        load_h(1)
+        nc.sync.dma_start(out=whh_sb[:, 2, :, :], in_=whh_v[:, :, 2, :])
+        load_cat(1)
+        nc.sync.dma_start(out=whh_sb[:, 3, :, :], in_=whh_v[:, :, 3, :])
         nc.sync.dma_start(out=wih_sb[:, 2, :, 0:IN], in_=wih_v[:, 2, :, :])
         nc.sync.dma_start(out=xr[0:1, :], in_=xf.unsqueeze(0))
         nc.sync.dma_start(out=xr[1:2, 0:2 * B - 1], in_=xf[1:2 * B].unsqueeze(0))
-        load(1)
+        load_xb(1)
 
         nc.gpsimd.tensor_scalar(out=xt[0:2, :], in0=xr[:, 0:2 * B:2], scalar1=1.0, scalar2=0.0, op0=ALU.mult, op1=ALU.add)
-        banks = whh_t(0)
-        grp = whh_c(0, banks, (nc.vector, nc.scalar))
-        ph0 = h_t(0, 0)
-        ph1 = h_t(0, 1, "gi")
-        h_c(0, 0, ph0)
-        h_c(0, 1, ph1)
-        whh_q(0, grp)
         pc = cat_t(0, "gh")
         cat_c(0, pc)
-        pw = wih_t(0, "gh")
+        pw = wih_t(0, "gi")
+        wih_c(0, pw, False)
+        banks = whh_t(0)
+        grp = whh_c(0, banks, (nc.vector, nc.scalar))
+        ph = h_t(0, 0)
+        h_c(0, 0, ph)
+        whh_q(0, grp)
         psx = bank("gh", [P, P])
         nc.tensor.transpose(psx[:], xrow[:].bitcast(F32), ident_f[:])
         psb = bank("px", [P, P], BF16)
         nc.tensor.transpose(psb[:], brow[:], ident_b[:])
-        h_q(0)
+        banks = whh_t(1)
         nc.vector.tensor_copy(out=xs[:], in_=psx[:, 0:32].bitcast(BF16).rearrange("p (t i) -> p t i", i=2))
-        wih_c(0, pw, False)
         nc.vector.tensor_copy(out=bias[:], in_=psb[:, 0:24])
+        h_q(0)
         nc.vector.tensor_tensor(out=brz[:], in0=bias[:, 0:8], in1=bias[:, 12:20], op=ALU.add)
         nc.vector.tensor_copy(out=wz0[:], in_=wih_sb[:, 1, :, 256:257].rearrange("p c i -> p (c i)"))
-        banks = whh_t(1)
         px_t(0)
         grps = {1: whh_c(1, banks, (nc.scalar, nc.scalar))}
 
@@ -218,70 +236,76 @@ def tile_wavernncell_pa_t_kernel(tc, x, feat, aux1, h, w_ih, w_hh, b_ih, b_hh, o
         acc = {}
         ts = {}
         opened = {}
-        late = []
+        slabs = {}
+        for b in range(NBLK):
+            for s in range(SIZES[b] // P):
+                at = 4 * (b + 1) + (2 * s if b == 0 else s)
+                slabs[at] = (STARTS[b] // P + s, b, s)
 
         def mm_mx(i, g):
-            blk, c = divmod(i, 4)
+            b, c = divmod(i, 4)
+            n = SIZES[b]
             q = c * 3 + g
             ps = bank("gh", [P, BB])
             nc.tensor.matmul_mx(
-                out=ps[:],
+                out=ps[:, 0:n],
                 lhsT=wc[:, q * P:(q + 1) * P].bitcast(FP8X4),
                 lhsT_scale=wsc[:, q * P:(q + 1) * P],
-                rhs=codes[blk][0][:].bitcast(FP8X4),
-                rhs_scale=codes[blk][1][:],
+                rhs=codes[b][0][:, 0:n].bitcast(FP8X4),
+                rhs_scale=codes[b][1][:, 0:n],
                 start=True,
                 stop=True,
             )
             return ps
 
         def mm_gi(i):
-            blk, c = divmod(i, 4)
+            b, c = divmod(i, 4)
+            n = SIZES[b]
             ps = bank("gi", [P, BB])
             for e in range(2):
-                nc.tensor.matmul(ps[:], lhsT=wt[:, e, 0, c * P:(c + 1) * P], rhs=catts[blk][:, e, :], start=(e == 0), stop=(e == 1))
+                nc.tensor.matmul(ps[:, 0:n], lhsT=wt[:, e, 0, c * P:(c + 1) * P], rhs=catts[b][:, e, 0:n], start=(e == 0), stop=(e == 1))
             gis[i] = ps
 
         def r1(i):
-            blk, c = divmod(i, 4)
+            b, c = divmod(i, 4)
+            n = SIZES[b]
             acc[i] = ew.tile([P, BB], F32, tag="a", name="a")
-            nc.vector.scalar_tensor_tensor(out=acc[i][:], in0=xbs[blk][:, :, 0], scalar=wih_sb[:, 0, c, 256:257], in1=gis[i][:], op0=ALU.mult, op1=ALU.add)
+            nc.vector.scalar_tensor_tensor(out=acc[i][:, 0:n], in0=xbs[b][:, 0:n, 0], scalar=wih_sb[:, 0, c, 256:257], in1=gis[i][:, 0:n], op0=ALU.mult, op1=ALU.add)
 
         def r2(i):
-            blk, c = divmod(i, 4)
-            nc.vector.scalar_tensor_tensor(out=acc[i][:], in0=pxs[blk][:], scalar=wih_sb[:, 0, c, 257:258], in1=acc[i][:], op0=ALU.mult, op1=ALU.add)
+            b, c = divmod(i, 4)
+            n = SIZES[b]
+            a = acc[i][:, 0:n]
+            nc.vector.scalar_tensor_tensor(out=a, in0=pxs[b][:, 0:n], scalar=wih_sb[:, 0, c, 257:258], in1=a, op0=ALU.mult, op1=ALU.add)
 
         def z_term(i):
-            blk, c = divmod(i, 4)
+            b, c = divmod(i, 4)
+            n = SIZES[b]
             ts[i] = ew.tile([P, BB], F32, tag="t", name="t")
-            nc.scalar.activation(out=ts[i][:], in_=xbs[blk][:, :, 0], func=ACT.Identity, scale=wz0[:, c:c + 1])
+            nc.scalar.activation(out=ts[i][:, 0:n], in_=xbs[b][:, 0:n, 0], func=ACT.Identity, scale=wz0[:, c:c + 1])
 
-        def open_sums(k):
-            kb, ks = divmod(k, 4)
-            tok = slice(ks * P, (ks + 1) * P)
+        def open_sums(k, b, s):
+            tok = slice(s * P, (s + 1) * P)
             ps_z = bank("z", [P, H])
-            nc.tensor.matmul(ps_z[:], lhsT=catts[kb][:, 0, tok], rhs=wt[:, 0, 1, :], start=True, stop=False)
+            nc.tensor.matmul(ps_z[:], lhsT=catts[b][:, 0, tok], rhs=wt[:, 0, 1, :], start=True, stop=False)
             ps_n = bank("n", [P, H])
             nc.tensor.matmul(ps_n[:], lhsT=xt[:, k * P:(k + 1) * P], rhs=xw[:], start=True, stop=False)
-            nc.tensor.matmul(ps_n[:], lhsT=catts[kb][:, 0, tok], rhs=wt[:, 0, 2, :], start=False, stop=False)
+            nc.tensor.matmul(ps_n[:], lhsT=catts[b][:, 0, tok], rhs=wt[:, 0, 2, :], start=False, stop=False)
             for ps, parts in ((ps_z, zts), (ps_n, vs)):
                 for c in range(4):
-                    nc.tensor.matmul(ps[:, c * P:(c + 1) * P], lhsT=parts[kb * 4 + c][:, tok], rhs=ident_f[:], is_transpose=True, start=False, stop=False)
+                    nc.tensor.matmul(ps[:, c * P:(c + 1) * P], lhsT=parts[b * 4 + c][:, tok], rhs=ident_f[:], is_transpose=True, start=False, stop=False)
             opened[k] = (ps_z, ps_n)
 
-        def close_sums(k):
-            kb, ks = divmod(k, 4)
-            tok = slice(ks * P, (ks + 1) * P)
+        def close_sums(k, b, s):
+            tok = slice(s * P, (s + 1) * P)
             for g, ps in enumerate(opened[k]):
-                nc.tensor.matmul(ps[:], lhsT=catts[kb][:, 1, tok], rhs=wt[:, 1, 1 + g, :], start=False, stop=True)
+                nc.tensor.matmul(ps[:], lhsT=catts[b][:, 1, tok], rhs=wt[:, 1, 1 + g, :], start=False, stop=True)
 
-        def blend(k, w, n, z):
-            blk, s = divmod(k, 4)
+        def blend(eng, k, w, b, s, n, z):
             d = ew.tile([P, 2, H], F32, tag="d", name="d", bufs=6)
-            eng = nc.vector if w == 1 else nc.gpsimd
             i = k % 2
             dd, nn, zz = (t[:, i:i + w, :] for t in (d, n, z))
-            eng.tensor_tensor(out=dd, in0=hs_[blk][:, s:s + w, :], in1=nn, op=ALU.subtract)
+            eng.tensor_tensor(out=dd, in0=hs_[b][:, s:s + w, :], in1=nn, op=ALU.subtract)
             eng.tensor_tensor(out=dd, in0=dd, in1=zz, op=ALU.mult)
             eng.tensor_tensor(out=dd, in0=dd, in1=nn, op=ALU.add)
             nc.sync.dma_start(out=out[k * P:(k + w) * P, :].rearrange("(s p) k -> p s k", p=P), in_=dd)
@@ -291,42 +315,51 @@ def tile_wavernncell_pa_t_kernel(tc, x, feat, aux1, h, w_ih, w_hh, b_ih, b_hh, o
         z_term(0)
         r2(0)
 
-        for j in range(NU + LAG):
+        late = None
+        for j in range(max(slabs) + 2):
             blk, c = divmod(j, 4)
             live = j < NU
             lag = 1 <= j <= NU
-            k = j - LAG
+            more = j + 1 < NU
             nxt = blk + 1
+            stage_next = live and nxt < NBLK
+            m = SIZES[blk] if live else 0
+            closing = slabs.get(j - 1)
+            opening = slabs.get(j)
             if live and c == 0 and blk + 2 < NBLK:
-                load(blk + 2)
-            if k >= 0:
-                close_sums(k)
+                load_h(blk + 2)
+                load_cat(blk + 2)
+                load_xb(blk + 2)
+            if closing:
+                close_sums(*closing)
             if lag:
                 gh_n = mm_mx(j - 1, 2)
             if live:
                 gh_r = mm_mx(j, 0)
                 gh_z = mm_mx(j, 1)
-            if j + 1 < NU:
+            if more:
                 mm_gi(j + 1)
             if j < 3:
                 whh_q(j + 1, grps[j + 1])
-            if k >= 0:
+            if closing:
+                k, kb, ks = closing
                 if k % 2 == 0:
                     n = ew.tile([P, 2, H], F32, tag="n", name="n", bufs=4)
-                    z = ew.tile([P, 2, H], F32, tag="z", name="z")
+                    z = ew.tile([P, 2, H], F32, tag="z", name="z", bufs=3)
                 nc.scalar.activation(out=n[:, k % 2, :], in_=opened[k][1][:], func=ACT.Tanh)
                 az = ew.tile([P, H], F32, tag="az", name="az")
                 nc.vector.scalar_tensor_tensor(out=az[:], in0=wz1[:], scalar=xs[:, k, 1:2], in1=opened[k][0][:], op0=ALU.mult, op1=ALU.add)
             if lag:
-                cn = (j - 1) % 4
+                pb, pcn = divmod(j - 1, 4)
+                pn = SIZES[pb]
                 v = ew.tile([P, BB], F32, tag="v", name="v", bufs=10)
-                nc.vector.scalar_tensor_tensor(out=v[:], in0=gh_n[:], scalar=bias[:, 20 + cn:21 + cn], in1=rs[j - 1][:], op0=ALU.add, op1=ALU.mult)
+                nc.vector.scalar_tensor_tensor(out=v[:, 0:pn], in0=gh_n[:, 0:pn], scalar=bias[:, 20 + pcn:21 + pcn], in1=rs[j - 1][:, 0:pn], op0=ALU.add, op1=ALU.mult)
                 vs[j - 1] = v
-            if 0 <= k + 1 < NU:
-                open_sums(k + 1)
+            if opening:
+                open_sums(*opening)
             ps_i = None
-            if live and nxt < NBLK:
-                if c < 2:
+            if stage_next:
+                if c < SIZES[nxt] // 256:
                     ps_i = h_t(nxt, c)
                 elif c == 2:
                     ps_i = cat_t(nxt)
@@ -342,32 +375,36 @@ def tile_wavernncell_pa_t_kernel(tc, x, feat, aux1, h, w_ih, w_hh, b_ih, b_hh, o
                 pw1 = wih_t(1, "z")
                 pw2 = wih_t(2, "n")
             if live:
-                nc.vector.tensor_tensor(out=acc[j][:], in0=gh_r[:], in1=acc[j][:], op=ALU.add)
-            if j + 1 < NU:
+                a = acc[j][:, 0:m]
+                nc.vector.tensor_tensor(out=a, in0=gh_r[:, 0:m], in1=a, op=ALU.add)
+            if more:
                 r1(j + 1)
             if live:
                 zt = ew.tile([P, BB], F32, tag="zt", name="zt", bufs=10)
-                nc.vector.scalar_tensor_tensor(out=zt[:], in0=gh_z[:], scalar=brz[:, 4 + c:5 + c], in1=ts[j][:], op0=ALU.add, op1=ALU.add)
+                nc.vector.scalar_tensor_tensor(out=zt[:, 0:m], in0=gh_z[:, 0:m], scalar=brz[:, 4 + c:5 + c], in1=ts[j][:, 0:m], op0=ALU.add, op1=ALU.add)
                 zts[j] = zt
-            if live and c == 3 and nxt < NBLK:
+            if stage_next and c == 3:
                 px_t(nxt)
-            if j + 1 < NU:
+            if more:
                 r2(j + 1)
-            if k >= 0:
+            if closing:
                 nc.scalar.activation(out=z[:, k % 2, :], in_=az[:], func=ACT.Sigmoid)
             if live:
                 r = ew.tile([P, BB], F32, tag="r", name="r")
-                nc.scalar.activation(out=r[:], in_=acc[j][:], func=ACT.Sigmoid, bias=brz[:, c:c + 1], scale=1.0)
+                nc.scalar.activation(out=r[:, 0:m], in_=a, func=ACT.Sigmoid, bias=brz[:, c:c + 1], scale=1.0)
                 rs[j] = r
-            if j + 1 < NU:
+            if more:
                 z_term(j + 1)
             if ps_i is not None:
                 if c == 2:
                     cat_c(nxt, ps_i)
                 else:
                     h_c(nxt, c, ps_i)
-            if live and c == 2 and nxt < NBLK:
+            if stage_next and c == 2:
                 h_q(nxt)
+            fb, fh = divmod(j + 1, 4)
+            if 2 <= fb + 1 < NBLK and fh < SIZES[fb + 1] // 256:
+                h_p(fb + 1, fh)
             if j == 0:
                 nc.vector.tensor_copy(out=t4[:, :, 0:2], in_=wih_sb[:, 2, :, 256:258])
                 nc.vector.tensor_copy(out=t4[:, :, 2], in_=bias[:, 8:12])
@@ -377,15 +414,16 @@ def tile_wavernncell_pa_t_kernel(tc, x, feat, aux1, h, w_ih, w_hh, b_ih, b_hh, o
                 nc.scalar.copy(out=wz1[:], in_=pz[:])
                 nc.scalar.copy(out=xw[:], in_=pxw[:].rearrange("p c m -> p (c m)"))
             if j == 3:
-                wih_c(1, pw1, True)
+                wih_c(1, pw1, False)
                 wih_c(2, pw2, True)
-            if k >= 0:
-                if k >= NU - 4:
-                    late.append((k, n, z))
-                    if len(late) > 1:
-                        kl, nl, zl = late[-2]
-                        blend(kl, 1, nl, zl)
+            if late:
+                blend(nc.vector, *late)
+                late = None
+            if closing:
+                if k >= VEC_FROM:
+                    late = (k, 1, kb, ks, n, z)
+                elif k + 1 == VEC_FROM and k % 2 == 0:
+                    blend(nc.gpsimd, k, 1, kb, ks, n, z)
                 elif k % 2 == 1:
-                    blend(k - 1, 2, n, z)
-        kl, nl, zl = late[-1]
-        blend(kl, 1, nl, zl)
+                    blend(nc.gpsimd, k - 1, 2, kb, ks - 1, n, z)
+        blend(nc.vector, *late)

@@ -21,7 +21,7 @@ STARTS = [sum(SIZES[:b]) for b in range(len(SIZES))]
 NBLK = len(SIZES)
 NU = NBLK * 4
 NSLAB = B // P
-VEC_FROM = NSLAB - 4
+VEC_FROM = NSLAB - 6
 WROW = 264
 FLOPS = 2 * B * 3 * H * (H + IN)
 
@@ -206,7 +206,6 @@ def tile_wavernncell_pa_t_kernel(tc, x, feat, aux1, h, w_ih, w_hh, b_ih, b_hh, o
         nc.sync.dma_start(out=xr[1:2, 0:2 * B - 1], in_=xf[1:2 * B].unsqueeze(0))
         load_xb(1)
 
-        nc.gpsimd.tensor_scalar(out=xt[0:2, :], in0=xr[:, 0:2 * B:2], scalar1=1.0, scalar2=0.0, op0=ALU.mult, op1=ALU.add)
         pc = cat_t(0, "gh")
         cat_c(0, pc)
         pw = wih_t(0, "gi")
@@ -236,11 +235,13 @@ def tile_wavernncell_pa_t_kernel(tc, x, feat, aux1, h, w_ih, w_hh, b_ih, b_hh, o
         acc = {}
         ts = {}
         opened = {}
+        queue = []
+        done = [0]
         slabs = {}
         for b in range(NBLK):
             for s in range(SIZES[b] // P):
-                at = 4 * (b + 1) + (2 * s if b == 0 else s)
-                slabs[at] = (STARTS[b] // P + s, b, s)
+                at = 4 * (b + 1) + (2 * s if b == 0 else 0 if b == NBLK - 1 else s)
+                slabs.setdefault(at, []).append((STARTS[b] // P + s, b, s))
 
         def mm_mx(i, g):
             b, c = divmod(i, 4)
@@ -286,9 +287,10 @@ def tile_wavernncell_pa_t_kernel(tc, x, feat, aux1, h, w_ih, w_hh, b_ih, b_hh, o
 
         def open_sums(k, b, s):
             tok = slice(s * P, (s + 1) * P)
-            ps_z = bank("z", [P, H])
+            last = k == NSLAB - 1
+            ps_z = bank("gi" if last else "z", [P, H])
             nc.tensor.matmul(ps_z[:], lhsT=catts[b][:, 0, tok], rhs=wt[:, 0, 1, :], start=True, stop=False)
-            ps_n = bank("n", [P, H])
+            ps_n = bank("tp" if last else "n", [P, H])
             nc.tensor.matmul(ps_n[:], lhsT=xt[:, k * P:(k + 1) * P], rhs=xw[:], start=True, stop=False)
             nc.tensor.matmul(ps_n[:], lhsT=catts[b][:, 0, tok], rhs=wt[:, 0, 2, :], start=False, stop=False)
             for ps, parts in ((ps_z, zts), (ps_n, vs)):
@@ -305,17 +307,28 @@ def tile_wavernncell_pa_t_kernel(tc, x, feat, aux1, h, w_ih, w_hh, b_ih, b_hh, o
             d = ew.tile([P, 2, H], F32, tag="d", name="d", bufs=6)
             i = k % 2
             dd, nn, zz = (t[:, i:i + w, :] for t in (d, n, z))
-            eng.tensor_tensor(out=dd, in0=hs_[b][:, s:s + w, :], in1=nn, op=ALU.subtract)
-            eng.tensor_tensor(out=dd, in0=dd, in1=zz, op=ALU.mult)
-            eng.tensor_tensor(out=dd, in0=dd, in1=nn, op=ALU.add)
-            nc.sync.dma_start(out=out[k * P:(k + w) * P, :].rearrange("(s p) k -> p s k", p=P), in_=dd)
+
+            def finish():
+                eng.tensor_tensor(out=dd, in0=dd, in1=nn, op=ALU.add)
+                nc.sync.dma_start(out=out[k * P:(k + w) * P, :].rearrange("(s p) k -> p s k", p=P), in_=dd)
+
+            return [
+                lambda: eng.tensor_tensor(out=dd, in0=hs_[b][:, s:s + w, :], in1=nn, op=ALU.subtract),
+                lambda: eng.tensor_tensor(out=dd, in0=dd, in1=zz, op=ALU.mult),
+                finish,
+            ]
+
+        def fill(count):
+            todo = queue[done[0]:done[0] + count]
+            done[0] += len(todo)
+            for step in todo:
+                step()
 
         mm_gi(0)
         r1(0)
         z_term(0)
         r2(0)
 
-        late = None
         for j in range(max(slabs) + 2):
             blk, c = divmod(j, 4)
             live = j < NU
@@ -324,14 +337,14 @@ def tile_wavernncell_pa_t_kernel(tc, x, feat, aux1, h, w_ih, w_hh, b_ih, b_hh, o
             nxt = blk + 1
             stage_next = live and nxt < NBLK
             m = SIZES[blk] if live else 0
-            closing = slabs.get(j - 1)
-            opening = slabs.get(j)
+            closing = slabs.get(j - 1, [])
+            opening = slabs.get(j, [])
             if live and c == 0 and blk + 2 < NBLK:
                 load_h(blk + 2)
                 load_cat(blk + 2)
                 load_xb(blk + 2)
-            if closing:
-                close_sums(*closing)
+            for slab in closing:
+                close_sums(*slab)
             if lag:
                 gh_n = mm_mx(j - 1, 2)
             if live:
@@ -341,22 +354,22 @@ def tile_wavernncell_pa_t_kernel(tc, x, feat, aux1, h, w_ih, w_hh, b_ih, b_hh, o
                 mm_gi(j + 1)
             if j < 3:
                 whh_q(j + 1, grps[j + 1])
-            if closing:
-                k, kb, ks = closing
+            azs = {}
+            for k, kb, ks in closing:
                 if k % 2 == 0:
                     n = ew.tile([P, 2, H], F32, tag="n", name="n", bufs=4)
                     z = ew.tile([P, 2, H], F32, tag="z", name="z", bufs=3)
                 nc.scalar.activation(out=n[:, k % 2, :], in_=opened[k][1][:], func=ACT.Tanh)
-                az = ew.tile([P, H], F32, tag="az", name="az")
-                nc.vector.scalar_tensor_tensor(out=az[:], in0=wz1[:], scalar=xs[:, k, 1:2], in1=opened[k][0][:], op0=ALU.mult, op1=ALU.add)
+                azs[k] = ew.tile([P, H], F32, tag="az", name="az")
+                nc.vector.scalar_tensor_tensor(out=azs[k][:], in0=wz1[:], scalar=xs[:, k, 1:2], in1=opened[k][0][:], op0=ALU.mult, op1=ALU.add)
             if lag:
                 pb, pcn = divmod(j - 1, 4)
                 pn = SIZES[pb]
                 v = ew.tile([P, BB], F32, tag="v", name="v", bufs=10)
                 nc.vector.scalar_tensor_tensor(out=v[:, 0:pn], in0=gh_n[:, 0:pn], scalar=bias[:, 20 + pcn:21 + pcn], in1=rs[j - 1][:, 0:pn], op0=ALU.add, op1=ALU.mult)
                 vs[j - 1] = v
-            if opening:
-                open_sums(*opening)
+            for slab in opening:
+                open_sums(*slab)
             ps_i = None
             if stage_next:
                 if c < SIZES[nxt] // 256:
@@ -387,14 +400,17 @@ def tile_wavernncell_pa_t_kernel(tc, x, feat, aux1, h, w_ih, w_hh, b_ih, b_hh, o
                 px_t(nxt)
             if more:
                 r2(j + 1)
-            if closing:
-                nc.scalar.activation(out=z[:, k % 2, :], in_=az[:], func=ACT.Sigmoid)
+            for k, kb, ks in closing:
+                nc.scalar.activation(out=z[:, k % 2, :], in_=azs[k][:], func=ACT.Sigmoid)
             if live:
                 r = ew.tile([P, BB], F32, tag="r", name="r")
                 nc.scalar.activation(out=r[:, 0:m], in_=a, func=ACT.Sigmoid, bias=brz[:, c:c + 1], scale=1.0)
                 rs[j] = r
             if more:
                 z_term(j + 1)
+            if live and c == 3:
+                lo, hi = STARTS[blk], STARTS[blk] + m
+                nc.scalar.copy(out=xt[0:2, lo:hi], in_=xr[:, 2 * lo:2 * hi:2])
             if ps_i is not None:
                 if c == 2:
                     cat_c(nxt, ps_i)
@@ -405,7 +421,7 @@ def tile_wavernncell_pa_t_kernel(tc, x, feat, aux1, h, w_ih, w_hh, b_ih, b_hh, o
             fb, fh = divmod(j + 1, 4)
             if 2 <= fb + 1 < NBLK and fh < SIZES[fb + 1] // 256:
                 h_p(fb + 1, fh)
-            if j == 0:
+            if j == 1:
                 nc.vector.tensor_copy(out=t4[:, :, 0:2], in_=wih_sb[:, 2, :, 256:258])
                 nc.vector.tensor_copy(out=t4[:, :, 2], in_=bias[:, 8:12])
             if j < 2:
@@ -416,14 +432,14 @@ def tile_wavernncell_pa_t_kernel(tc, x, feat, aux1, h, w_ih, w_hh, b_ih, b_hh, o
             if j == 3:
                 wih_c(1, pw1, False)
                 wih_c(2, pw2, True)
-            if late:
-                blend(nc.vector, *late)
-                late = None
-            if closing:
+            fill(2 if live else 3)
+            for k, kb, ks in closing:
                 if k >= VEC_FROM:
-                    late = (k, 1, kb, ks, n, z)
-                elif k + 1 == VEC_FROM and k % 2 == 0:
-                    blend(nc.gpsimd, k, 1, kb, ks, n, z)
+                    queue += blend(nc.vector, k, 1, kb, ks, n, z)
                 elif k % 2 == 1:
-                    blend(nc.gpsimd, k - 1, 2, kb, ks - 1, n, z)
-        blend(nc.vector, *late)
+                    for step in blend(nc.gpsimd, k - 1, 2, kb, ks - 1, n, z):
+                        step()
+            if j == NU:
+                fill(len(queue) - done[0])
+        for i in (-6, -3, -5, -2, -4, -1):
+            queue[i]()

@@ -61,7 +61,7 @@ def tile_wavernncell_pa_t_kernel(tc, x, feat, aux1, h, w_ih, w_hh, b_ih, b_hh, o
         wih_sb = const.tile([P, 3, 4, WROW], BF16, name="wih_sb")
         wc = const.tile([P, 12 * P], U32, name="wc", align_bytes=64)
         wsc = const.tile([P, 12 * P], U8, name="wsc", align_bytes=64)
-        wt = const.tile([P, 2, 3, H], BF16, name="wt")
+        wt = [const.tile([P, 2, H], BF16, name=name) for name in ("wt_r", "wt_z", "wt_n")]
         wz0 = const.tile([P, 4], F32, name="wz0")
         wz1 = const.tile([P, H], BF16, name="wz1")
         xw = const.tile([P, H], BF16, name="xw")
@@ -183,9 +183,9 @@ def tile_wavernncell_pa_t_kernel(tc, x, feat, aux1, h, w_ih, w_hh, b_ih, b_hh, o
         def wih_c(g, ps, on_scalar):
             src = ps[:].rearrange("w c m -> w (c m)").bitcast(BF16).rearrange("w (m e) -> w e m", e=2)
             if on_scalar:
-                nc.scalar.copy(out=wt[:, :, g, :], in_=src)
+                nc.scalar.copy(out=wt[g][:], in_=src)
             else:
-                nc.vector.tensor_copy(out=wt[:, :, g, :], in_=src)
+                nc.vector.tensor_copy(out=wt[g][:], in_=src)
 
         load_cat(0)
         nc.sync.dma_start(out=wih_sb[:, 0, :, 0:IN], in_=wih_v[:, 0, :, :])
@@ -217,13 +217,9 @@ def tile_wavernncell_pa_t_kernel(tc, x, feat, aux1, h, w_ih, w_hh, b_ih, b_hh, o
         whh_q(0, grp)
         psx = bank("gh", [P, P])
         nc.tensor.transpose(psx[:], xrow[:].bitcast(F32), ident_f[:])
-        psb = bank("px", [P, P], BF16)
-        nc.tensor.transpose(psb[:], brow[:], ident_b[:])
         banks = whh_t(1)
         nc.vector.tensor_copy(out=xs[:], in_=psx[:, 0:32].bitcast(BF16).rearrange("p (t i) -> p t i", i=2))
-        nc.vector.tensor_copy(out=bias[:], in_=psb[:, 0:24])
         h_q(0)
-        nc.vector.tensor_tensor(out=brz[:], in0=bias[:, 0:8], in1=bias[:, 12:20], op=ALU.add)
         nc.vector.tensor_copy(out=wz0[:], in_=wih_sb[:, 1, :, 256:257].rearrange("p c i -> p (c i)"))
         px_t(0)
         grps = {1: whh_c(1, banks, (nc.scalar, nc.scalar))}
@@ -264,7 +260,7 @@ def tile_wavernncell_pa_t_kernel(tc, x, feat, aux1, h, w_ih, w_hh, b_ih, b_hh, o
             n = SIZES[b]
             ps = bank("gi", [P, BB])
             for e in range(2):
-                nc.tensor.matmul(ps[:, 0:n], lhsT=wt[:, e, 0, c * P:(c + 1) * P], rhs=catts[b][:, e, 0:n], start=(e == 0), stop=(e == 1))
+                nc.tensor.matmul(ps[:, 0:n], lhsT=wt[0][:, e, c * P:(c + 1) * P], rhs=catts[b][:, e, 0:n], start=(e == 0), stop=(e == 1))
             gis[i] = ps
 
         def r1(i):
@@ -289,10 +285,10 @@ def tile_wavernncell_pa_t_kernel(tc, x, feat, aux1, h, w_ih, w_hh, b_ih, b_hh, o
             tok = slice(s * P, (s + 1) * P)
             last = k == NSLAB - 1
             ps_z = bank("gi" if last else "z", [P, H])
-            nc.tensor.matmul(ps_z[:], lhsT=catts[b][:, 0, tok], rhs=wt[:, 0, 1, :], start=True, stop=False)
+            nc.tensor.matmul(ps_z[:], lhsT=catts[b][:, 0, tok], rhs=wt[1][:, 0, :], start=True, stop=False)
             ps_n = bank("tp" if last else "n", [P, H])
             nc.tensor.matmul(ps_n[:], lhsT=xt[:, k * P:(k + 1) * P], rhs=xw[:], start=True, stop=False)
-            nc.tensor.matmul(ps_n[:], lhsT=catts[b][:, 0, tok], rhs=wt[:, 0, 2, :], start=False, stop=False)
+            nc.tensor.matmul(ps_n[:], lhsT=catts[b][:, 0, tok], rhs=wt[2][:, 0, :], start=False, stop=False)
             for ps, parts in ((ps_z, zts), (ps_n, vs)):
                 for c in range(4):
                     nc.tensor.matmul(ps[:, c * P:(c + 1) * P], lhsT=parts[b * 4 + c][:, tok], rhs=ident_f[:], is_transpose=True, start=False, stop=False)
@@ -301,7 +297,7 @@ def tile_wavernncell_pa_t_kernel(tc, x, feat, aux1, h, w_ih, w_hh, b_ih, b_hh, o
         def close_sums(k, b, s):
             tok = slice(s * P, (s + 1) * P)
             for g, ps in enumerate(opened[k]):
-                nc.tensor.matmul(ps[:], lhsT=catts[b][:, 1, tok], rhs=wt[:, 1, 1 + g, :], start=False, stop=True)
+                nc.tensor.matmul(ps[:], lhsT=catts[b][:, 1, tok], rhs=wt[1 + g][:, 1, :], start=False, stop=True)
 
         def blend(eng, k, w, b, s, n, z):
             d = ew.tile([P, 2, H], F32, tag="d", name="d", bufs=6)
@@ -325,9 +321,13 @@ def tile_wavernncell_pa_t_kernel(tc, x, feat, aux1, h, w_ih, w_hh, b_ih, b_hh, o
                 step()
 
         mm_gi(0)
+        psb = bank("tp", [P, P], BF16)
+        nc.tensor.transpose(psb[:], brow[:], ident_b[:])
         r1(0)
         z_term(0)
+        nc.vector.tensor_copy(out=bias[:], in_=psb[:, 0:24])
         r2(0)
+        nc.vector.tensor_tensor(out=brz[:], in0=bias[:, 0:8], in1=bias[:, 12:20], op=ALU.add)
 
         for j in range(max(slabs) + 2):
             blk, c = divmod(j, 4)
@@ -425,7 +425,7 @@ def tile_wavernncell_pa_t_kernel(tc, x, feat, aux1, h, w_ih, w_hh, b_ih, b_hh, o
                 nc.vector.tensor_copy(out=t4[:, :, 0:2], in_=wih_sb[:, 2, :, 256:258])
                 nc.vector.tensor_copy(out=t4[:, :, 2], in_=bias[:, 8:12])
             if j < 2:
-                grps[j + 2] = whh_c(j + 2, banks, (nc.scalar, nc.scalar))
+                grps[j + 2] = whh_c(j + 2, banks, (nc.vector, nc.scalar))
             if j == 2:
                 nc.scalar.copy(out=wz1[:], in_=pz[:])
                 nc.scalar.copy(out=xw[:], in_=pxw[:].rearrange("p c m -> p (c m)"))

@@ -285,19 +285,20 @@ def tile_wavernncell_pa_t_kernel(tc, x, feat, aux1, h, w_ih, w_hh, b_ih, b_hh, o
             tok = slice(s * P, (s + 1) * P)
             last = k == NSLAB - 1
             ps_z = bank("gi" if last else "z", [P, H])
-            nc.tensor.matmul(ps_z[:], lhsT=catts[b][:, 0, tok], rhs=wt[1][:, 0, :], start=True, stop=False)
             ps_n = bank("tp" if last else "n", [P, H])
-            nc.tensor.matmul(ps_n[:], lhsT=xt[:, k * P:(k + 1) * P], rhs=xw[:], start=True, stop=False)
-            nc.tensor.matmul(ps_n[:], lhsT=catts[b][:, 0, tok], rhs=wt[2][:, 0, :], start=False, stop=False)
             for ps, parts in ((ps_z, zts), (ps_n, vs)):
                 for c in range(4):
-                    nc.tensor.matmul(ps[:, c * P:(c + 1) * P], lhsT=parts[b * 4 + c][:, tok], rhs=ident_f[:], is_transpose=True, start=False, stop=False)
+                    nc.tensor.matmul(ps[:, c * P:(c + 1) * P], lhsT=parts[b * 4 + c][:, tok], rhs=ident_f[:], is_transpose=True, start=(c == 0), stop=False)
             opened[k] = (ps_z, ps_n)
 
         def close_sums(k, b, s):
             tok = slice(s * P, (s + 1) * P)
-            for g, ps in enumerate(opened[k]):
-                nc.tensor.matmul(ps[:], lhsT=catts[b][:, 1, tok], rhs=wt[1 + g][:, 1, :], start=False, stop=True)
+            ps_z, ps_n = opened[k]
+            for e in range(2):
+                nc.tensor.matmul(ps_z[:], lhsT=catts[b][:, e, tok], rhs=wt[1][:, e, :], start=False, stop=(e == 1))
+            nc.tensor.matmul(ps_n[:], lhsT=xt[:, k * P:(k + 1) * P], rhs=xw[:], start=False, stop=False)
+            for e in range(2):
+                nc.tensor.matmul(ps_n[:], lhsT=catts[b][:, e, tok], rhs=wt[2][:, e, :], start=False, stop=(e == 1))
 
         def blend(eng, k, w, b, s, n, z):
             d = ew.tile([P, 2, H], F32, tag="d", name="d", bufs=6)

from contextlib import ExitStack

import concourse.mybir as mybir
from concourse.masks import make_identity

F32 = mybir.dt.float32
BF16 = mybir.dt.bfloat16
U32 = mybir.dt.uint32
U8 = mybir.dt.uint8
FP8X4 = mybir.dt.float8_e4m3fn_x4
ALU = mybir.AluOpType
ACT = mybir.ActivationFunctionType

P = 128
B = 4096
H = 512
IN = 258
BB = 512
SIZES = [256] + [BB] * 7 + [256]
STARTS = [sum(SIZES[:b]) for b in range(len(SIZES))]
NBLK = len(SIZES)
NU = NBLK * 4
NSLAB = B // P
VEC_FROM = NSLAB - 6
WROW = 264
FLOPS = 2 * B * 3 * H * (H + IN)


def tile_wavernncell_pa_t_kernel(tc, x, feat, aux1, h, w_ih, w_hh, b_ih, b_hh, out):
    nc = tc.nc
    with ExitStack() as ctx:
        const = ctx.enter_context(tc.tile_pool(name="const", bufs=1))
        ld = ctx.enter_context(tc.tile_pool(name="ld", bufs=3))
        stage = ctx.enter_context(tc.tile_pool(name="stage", bufs=3))
        ew = ctx.enter_context(tc.tile_pool(name="ew", bufs=2))
        psum = ctx.enter_context(tc.psum_pool(name="psum", bufs=1))
        ctx.enter_context(tc.manual_schedule())

        xf = x.rearrange("b i -> (b i)")
        whh_v = w_hh.rearrange("(g c m) k -> m g c k", g=3, m=P)
        wih_v = w_ih.rearrange("(g c m) k -> m g c k", g=3, m=P)

        warm = const.tile([P, 1], F32, name="warm")
        nc.vector.memset(warm[:], 0.0)
        nc.scalar.activation(out=warm[:], in_=warm[:], func=ACT.Sigmoid)
        ident_f = const.tile([P, P], F32, name="ident_f")
        make_identity(nc, ident_f[:])
        ident_b = const.tile([P, P], BF16, name="ident_b")
        make_identity(nc, ident_b[:])
        brow = const.tile([P, P], BF16, name="brow")
        nc.vector.memset(brow[:], 0.0)
        xrow = const.tile([P, 256], BF16, name="xrow")
        nc.vector.memset(xrow[:], 0.0)
        t4 = const.tile([P, 4, P], BF16, name="t4")
        nc.vector.memset(t4[:], 0.0)
        xt = const.tile([P, B], BF16, name="xt")
        nc.gpsimd.memset(xt[:], 1.0)
        xr = const.tile([2, 2 * B], BF16, name="xr")

        whh_sb = const.tile([P, 4, 3, H], BF16, name="whh_sb")
        wih_sb = const.tile([P, 3, 4, WROW], BF16, name="wih_sb")
        wc = const.tile([P, 12 * P], U32, name="wc", align_bytes=64)
        wsc = const.tile([P, 12 * P], U8, name="wsc", align_bytes=64)
        wt = [const.tile([P, 2, H], BF16, name=name) for name in ("wt_r", "wt_z", "wt_n")]
        wz0 = const.tile([P, 4], F32, name="wz0")
        wz1 = const.tile([P, H], BF16, name="wz1")
        xw = const.tile([P, H], BF16, name="xw")
        bias = const.tile([P, 24], F32, name="bias")
        brz = const.tile([P, 8], F32, name="brz")
        xs = const.tile([P, NSLAB, 2], BF16, name="xs")
        whh_w = whh_sb[:].bitcast(F32)
        wih_w = wih_sb[:].bitcast(F32)

        hs_ = {}
        cats = {}
        xbs = {}
        hgrps = {}
        codes = {}
        catts = {}
        pxs = {}
        perms = {}

        def bank(tag, shape, dtype=F32):
            return psum.tile(shape, dtype, tag=tag, name=tag, bufs=(3 if tag == "gh" else 1))

        def load_h(b):
            t0, n = STARTS[b], SIZES[b]
            hs_[b] = ld.tile([P, 4, H], BF16, tag="h", name="h_sb", bufs=5)
            nc.sync.dma_start(out=hs_[b][:, 0:n // P, :], in_=h[t0:t0 + n, :].rearrange("(s p) k -> p s k", p=P))

        def load_cat(b):
            t0, n = STARTS[b], SIZES[b]
            cats[b] = ld.tile([P, 4, 256], BF16, tag="cat", name="cat")
            nc.sync.dma_start(out=cats[b][:, 0:n // P, 0:128], in_=feat[t0:t0 + n, :].rearrange("(s p) k -> p s k", p=P))
            nc.sync.dma_start(out=cats[b][:, 0:n // P, 128:256], in_=aux1[t0:t0 + n, :].rearrange("(s p) k -> p s k", p=P))

        def load_xb(b):
            t0, n = STARTS[b], SIZES[b]
            xbs[b] = ld.tile([P, BB, 2], BF16, tag="xb", name="xb")
            nc.sync.dma_start(out=xbs[b][:, 0:n, :].rearrange("p b i -> p (b i)"), in_=xf[2 * t0:2 * (t0 + n)].partition_broadcast(P))

        def h_p(b, half):
            hp = stage.tile([P, 2, 2, P], F32, tag="hp", name="hp")
            hw = hs_[b][:].bitcast(F32)
            nc.scalar.copy(out=hp[:], in_=hw[:, half * 2:half * 2 + 2, :].rearrange("p s (w u) -> p s u w", u=2))
            perms[(b, half)] = hp

        def h_t(b, half, tag="tp"):
            ps = bank(tag, [P, 2, 2, P])
            hw = hs_[b][:].bitcast(F32)
            for s2 in range(2):
                for uu in range(2):
                    src = perms[(b, half)][:, s2, uu, :] if (b, half) in perms else hw[:, half * 2 + s2, uu:256:2]
                    nc.tensor.transpose(ps[:, uu, s2, :], src, ident_f[:])
            return ps

        def h_c(b, half, ps):
            if half == 0:
                hgrps[b] = stage.tile([P, 4 * BB], BF16, tag="hgrp", name="hgrp", bufs=2, align_bytes=64)
            dst = hgrps[b][:].bitcast(F32)[:, half * 512:(half + 1) * 512].rearrange("p (b u) -> p b u", u=2)
            nc.scalar.copy(out=dst, in_=ps[:].rearrange("p u s b -> p (s b) u"))

        def h_q(b):
            n = SIZES[b]
            hc = stage.tile([P, BB], U32, tag="hc", name="hc", align_bytes=64)
            hsc = stage.tile([P, BB], U8, tag="hsc", name="hsc", align_bytes=64)
            nc.vector.quantize_mx(out=hc[:, 0:n].bitcast(FP8X4), scales=hsc[:, 0:n], in_=hgrps[b][:, 0:4 * n])
            codes[b] = (hc, hsc)

        def cat_t(b, tag="tp"):
            ps = bank(tag, [P, 4, P])
            cw = cats[b][:].bitcast(F32)
            for s in range(SIZES[b] // P):
                nc.tensor.transpose(ps[:, s, :], cw[:, s, :], ident_f[:])
            return ps

        def cat_c(b, ps):
            n = SIZES[b]
            catts[b] = stage.tile([P, 2, BB], BF16, tag="catt", name="catt")
            src = ps[:].rearrange("w s b -> w (s b)")[:, 0:n].bitcast(BF16).rearrange("w (b e) -> w e b", e=2)
            nc.scalar.copy(out=catts[b][:, :, 0:n], in_=src)

        def px_t(b):
            px = bank("px", [P, BB], BF16)
            for s in range(SIZES[b] // P):
                nc.tensor.transpose(px[:, s * P:(s + 1) * P], xs[:, STARTS[b] // P + s, 1:2].to_broadcast([P, P]), ident_b[:])
            pxs[b] = px

        def whh_t(c):
            banks = []
            for tag, gs in (("z", (0, 1)), ("n", (2,))):
                ps = bank(tag, [P, len(gs), 2, P])
                for j, g in enumerate(gs):
                    for uu in range(2):
                        nc.tensor.transpose(ps[:, j, uu, :], whh_w[:, c, g, uu:256:2], ident_f[:])
                banks.append(ps)
            return banks

        def whh_c(c, banks, engines):
            grp = stage.tile([P, 3 * H], BF16, tag="wgrp", name="wgrp", bufs=3, align_bytes=64)
            w = grp[:].bitcast(F32)
            for j, ps in enumerate(banks):
                n = 2 - j
                dst = w[:, j * 512:j * 512 + n * 256].rearrange("p (g m u) -> p g m u", m=P, u=2)
                src = ps[:].rearrange("p g u m -> p g m u")
                if engines[j] is nc.scalar:
                    nc.scalar.copy(out=dst, in_=src)
                else:
                    nc.vector.tensor_copy(out=dst, in_=src)
            return grp

        def whh_q(c, grp):
            for lo, n in ((0, 2), (2, 1)):
                a, b = (c * 3 + lo) * P, (c * 3 + lo + n) * P
                nc.vector.quantize_mx(out=wc[:, a:b].bitcast(FP8X4), scales=wsc[:, a:b], in_=grp[:, lo * H:(lo + n) * H])

        def wih_t(g, tag):
            ps = bank(tag, [P, 4, P])
            for c in range(4):
                nc.tensor.transpose(ps[:, c, :], wih_w[:, g, c, 0:P], ident_f[:])
            return ps

        def wih_c(g, ps, on_scalar):
            src = ps[:].rearrange("w c m -> w (c m)").bitcast(BF16).rearrange("w (m e) -> w e m", e=2)
            if on_scalar:
                nc.scalar.copy(out=wt[g][:], in_=src)
            else:
                nc.vector.tensor_copy(out=wt[g][:], in_=src)

        load_cat(0)
        nc.sync.dma_start(out=wih_sb[:, 0, :, 0:IN], in_=wih_v[:, 0, :, :])
        nc.sync.dma_start(out=whh_sb[:, 0, :, :], in_=whh_v[:, :, 0, :])
        load_h(0)
        nc.scalar.dma_start(out=xrow[0:32, :], in_=xf.rearrange("(t c) -> t c", c=256))
        nc.scalar.dma_start(out=brow[0:12, :], in_=b_ih.rearrange("(r c) -> r c", c=P))
        nc.scalar.dma_start(out=brow[12:24, :], in_=b_hh.rearrange("(r c) -> r c", c=P))
        load_xb(0)
        nc.sync.dma_start(out=whh_sb[:, 1, :, :], in_=whh_v[:, :, 1, :])
        nc.sync.dma_start(out=wih_sb[:, 1, :, 0:IN], in_=wih_v[:, 1, :, :])
        load_h(1)
        nc.sync.dma_start(out=whh_sb[:, 2, :, :], in_=whh_v[:, :, 2, :])
        load_cat(1)
        nc.sync.dma_start(out=whh_sb[:, 3, :, :], in_=whh_v[:, :, 3, :])
        nc.sync.dma_start(out=wih_sb[:, 2, :, 0:IN], in_=wih_v[:, 2, :, :])
        nc.sync.dma_start(out=xr[0:1, :], in_=xf.unsqueeze(0))
        nc.sync.dma_start(out=xr[1:2, 0:2 * B - 1], in_=xf[1:2 * B].unsqueeze(0))
        load_xb(1)

        pc = cat_t(0, "gh")
        cat_c(0, pc)
        pw = wih_t(0, "gi")
        wih_c(0, pw, False)
        banks = whh_t(0)
        grp = whh_c(0, banks, (nc.vector, nc.scalar))
        ph = h_t(0, 0)
        h_c(0, 0, ph)
        whh_q(0, grp)
        psx = bank("gh", [P, P])
        nc.tensor.transpose(psx[:], xrow[:].bitcast(F32), ident_f[:])
        banks = whh_t(1)
        nc.vector.tensor_copy(out=xs[:], in_=psx[:, 0:32].bitcast(BF16).rearrange("p (t i) -> p t i", i=2))
        h_q(0)
        nc.vector.tensor_copy(out=wz0[:], in_=wih_sb[:, 1, :, 256:257].rearrange("p c i -> p (c i)"))
        px_t(0)
        grps = {1: whh_c(1, banks, (nc.scalar, nc.scalar))}

        rs = {}
        zts = {}
        vs = {}
        gis = {}
        acc = {}
        ts = {}
        opened = {}
        queue = []
        done = [0]
        slabs = {}
        for b in range(NBLK):
            for s in range(SIZES[b] // P):
                at = 4 * (b + 1) + (2 * s if b == 0 else 0 if b == NBLK - 1 else s)
                slabs.setdefault(at, []).append((STARTS[b] // P + s, b, s))

        def mm_mx(i, g):
            b, c = divmod(i, 4)
            n = SIZES[b]
            q = c * 3 + g
            ps = bank("gh", [P, BB])
            nc.tensor.matmul_mx(
                out=ps[:, 0:n],
                lhsT=wc[:, q * P:(q + 1) * P].bitcast(FP8X4),
                lhsT_scale=wsc[:, q * P:(q + 1) * P],
                rhs=codes[b][0][:, 0:n].bitcast(FP8X4),
                rhs_scale=codes[b][1][:, 0:n],
                start=True,
                stop=True,
            )
            return ps

        def mm_gi(i):
            b, c = divmod(i, 4)
            n = SIZES[b]
            ps = bank("gi", [P, BB])
            for e in range(2):
                nc.tensor.matmul(ps[:, 0:n], lhsT=wt[0][:, e, c * P:(c + 1) * P], rhs=catts[b][:, e, 0:n], start=(e == 0), stop=(e == 1))
            gis[i] = ps

        def r1(i):
            b, c = divmod(i, 4)
            n = SIZES[b]
            acc[i] = ew.tile([P, BB], F32, tag="a", name="a")
            nc.vector.scalar_tensor_tensor(out=acc[i][:, 0:n], in0=xbs[b][:, 0:n, 0], scalar=wih_sb[:, 0, c, 256:257], in1=gis[i][:, 0:n], op0=ALU.mult, op1=ALU.add)

        def r2(i):
            b, c = divmod(i, 4)
            n = SIZES[b]
            a = acc[i][:, 0:n]
            nc.vector.scalar_tensor_tensor(out=a, in0=pxs[b][:, 0:n], scalar=wih_sb[:, 0, c, 257:258], in1=a, op0=ALU.mult, op1=ALU.add)

        def z_term(i):
            b, c = divmod(i, 4)
            n = SIZES[b]
            ts[i] = ew.tile([P, BB], F32, tag="t", name="t")
            nc.scalar.activation(out=ts[i][:, 0:n], in_=xbs[b][:, 0:n, 0], func=ACT.Identity, scale=wz0[:, c:c + 1])

        def open_sums(k, b, s):
            tok = slice(s * P, (s + 1) * P)
            last = k == NSLAB - 1
            ps_z = bank("gi" if last else "z", [P, H])
            ps_n = bank("tp" if last else "n", [P, H])
            for ps, parts in ((ps_z, zts), (ps_n, vs)):
                for c in range(4):
                    nc.tensor.matmul(ps[:, c * P:(c + 1) * P], lhsT=parts[b * 4 + c][:, tok], rhs=ident_f[:], is_transpose=True, start=(c == 0), stop=False)
            opened[k] = (ps_z, ps_n)

        def close_sums(k, b, s):
            tok = slice(s * P, (s + 1) * P)
            ps_z, ps_n = opened[k]
            for e in range(2):
                nc.tensor.matmul(ps_z[:], lhsT=catts[b][:, e, tok], rhs=wt[1][:, e, :], start=False, stop=(e == 1))
            nc.tensor.matmul(ps_n[:], lhsT=xt[:, k * P:(k + 1) * P], rhs=xw[:], start=False, stop=False)
            for e in range(2):
                nc.tensor.matmul(ps_n[:], lhsT=catts[b][:, e, tok], rhs=wt[2][:, e, :], start=False, stop=(e == 1))

        def blend(eng, k, w, b, s, n, z):
            d = ew.tile([P, 2, H], F32, tag="d", name="d", bufs=6)
            i = k % 2
            dd, nn, zz = (t[:, i:i + w, :] for t in (d, n, z))

            def finish():
                eng.tensor_tensor(out=dd, in0=dd, in1=nn, op=ALU.add)
                nc.sync.dma_start(out=out[k * P:(k + w) * P, :].rearrange("(s p) k -> p s k", p=P), in_=dd)

            return [
                lambda: eng.tensor_tensor(out=dd, in0=hs_[b][:, s:s + w, :], in1=nn, op=ALU.subtract),
                lambda: eng.tensor_tensor(out=dd, in0=dd, in1=zz, op=ALU.mult),
                finish,
            ]

        def fill(count):
            todo = queue[done[0]:done[0] + count]
            done[0] += len(todo)
            for step in todo:
                step()

        mm_gi(0)
        psb = bank("tp", [P, P], BF16)
        nc.tensor.transpose(psb[:], brow[:], ident_b[:])
        r1(0)
        z_term(0)
        nc.vector.tensor_copy(out=bias[:], in_=psb[:, 0:24])
        r2(0)
        nc.vector.tensor_tensor(out=brz[:], in0=bias[:, 0:8], in1=bias[:, 12:20], op=ALU.add)

        for j in range(max(slabs) + 2):
            blk, c = divmod(j, 4)
            live = j < NU
            lag = 1 <= j <= NU
            more = j + 1 < NU
            nxt = blk + 1
            stage_next = live and nxt < NBLK
            m = SIZES[blk] if live else 0
            closing = slabs.get(j - 1, [])
            opening = slabs.get(j, [])
            if live and c == 0 and blk + 2 < NBLK:
                load_h(blk + 2)
                load_cat(blk + 2)
                load_xb(blk + 2)
            for slab in closing:
                close_sums(*slab)
            if lag:
                gh_n = mm_mx(j - 1, 2)
            if live:
                gh_r = mm_mx(j, 0)
                gh_z = mm_mx(j, 1)
            if more:
                mm_gi(j + 1)
            if j < 3:
                whh_q(j + 1, grps[j + 1])
            azs = {}
            for k, kb, ks in closing:
                if k % 2 == 0:
                    n = ew.tile([P, 2, H], F32, tag="n", name="n", bufs=4)
                    z = ew.tile([P, 2, H], F32, tag="z", name="z", bufs=3)
                nc.scalar.activation(out=n[:, k % 2, :], in_=opened[k][1][:], func=ACT.Tanh)
                azs[k] = ew.tile([P, H], F32, tag="az", name="az")
                nc.vector.scalar_tensor_tensor(out=azs[k][:], in0=wz1[:], scalar=xs[:, k, 1:2], in1=opened[k][0][:], op0=ALU.mult, op1=ALU.add)
            if lag:
                pb, pcn = divmod(j - 1, 4)
                pn = SIZES[pb]
                v = ew.tile([P, BB], F32, tag="v", name="v", bufs=10)
                nc.vector.scalar_tensor_tensor(out=v[:, 0:pn], in0=gh_n[:, 0:pn], scalar=bias[:, 20 + pcn:21 + pcn], in1=rs[j - 1][:, 0:pn], op0=ALU.add, op1=ALU.mult)
                vs[j - 1] = v
            for slab in opening:
                open_sums(*slab)
            ps_i = None
            if stage_next:
                if c < SIZES[nxt] // 256:
                    ps_i = h_t(nxt, c)
                elif c == 2:
                    ps_i = cat_t(nxt)
            if j < 2:
                banks = whh_t(j + 2)
            if j == 2:
                pz = bank("z", [P, H], BF16)
                pxw = bank("n", [P, 4, P], BF16)
                for cc in range(4):
                    nc.tensor.transpose(pz[:, cc * P:(cc + 1) * P], wih_sb[:, 1, cc, 257:258].to_broadcast([P, P]), ident_b[:])
                    nc.tensor.transpose(pxw[:, cc, :], t4[:, cc, :], ident_b[:])
            if j == 3:
                pw1 = wih_t(1, "z")
                pw2 = wih_t(2, "n")
            if live:
                a = acc[j][:, 0:m]
                nc.vector.tensor_tensor(out=a, in0=gh_r[:, 0:m], in1=a, op=ALU.add)
            if more:
                r1(j + 1)
            if live:
                zt = ew.tile([P, BB], F32, tag="zt", name="zt", bufs=10)
                nc.vector.scalar_tensor_tensor(out=zt[:, 0:m], in0=gh_z[:, 0:m], scalar=brz[:, 4 + c:5 + c], in1=ts[j][:, 0:m], op0=ALU.add, op1=ALU.add)
                zts[j] = zt
            if stage_next and c == 3:
                px_t(nxt)
            if more:
                r2(j + 1)
            for k, kb, ks in closing:
                nc.scalar.activation(out=z[:, k % 2, :], in_=azs[k][:], func=ACT.Sigmoid)
            if live:
                r = ew.tile([P, BB], F32, tag="r", name="r")
                nc.scalar.activation(out=r[:, 0:m], in_=a, func=ACT.Sigmoid, bias=brz[:, c:c + 1], scale=1.0)
                rs[j] = r
            if more:
                z_term(j + 1)
            if live and c == 3:
                lo, hi = STARTS[blk], STARTS[blk] + m
                nc.scalar.copy(out=xt[0:2, lo:hi], in_=xr[:, 2 * lo:2 * hi:2])
            if ps_i is not None:
                if c == 2:
                    cat_c(nxt, ps_i)
                else:
                    h_c(nxt, c, ps_i)
            if stage_next and c == 2:
                h_q(nxt)
            fb, fh = divmod(j + 1, 4)
            if 2 <= fb + 1 < NBLK and fh < SIZES[fb + 1] // 256:
                h_p(fb + 1, fh)
            if j == 1:
                nc.vector.tensor_copy(out=t4[:, :, 0:2], in_=wih_sb[:, 2, :, 256:258])
                nc.vector.tensor_copy(out=t4[:, :, 2], in_=bias[:, 8:12])
            if j < 2:
                grps[j + 2] = whh_c(j + 2, banks, (nc.vector, nc.scalar))
            if j == 2:
                nc.scalar.copy(out=wz1[:], in_=pz[:])
                nc.scalar.copy(out=xw[:], in_=pxw[:].rearrange("p c m -> p (c m)"))
            if j == 3:
                wih_c(1, pw1, False)
                wih_c(2, pw2, True)
            fill(2 if live else 3)
            for k, kb, ks in closing:
                if k >= VEC_FROM:
                    queue += blend(nc.vector, k, 1, kb, ks, n, z)
                elif k % 2 == 1:
                    for step in blend(nc.gpsimd, k - 1, 2, kb, ks - 1, n, z):
                        step()
            if j == NU:
                fill(len(queue) - done[0])
        for i in (-6, -3, -5, -2, -4, -1):
            queue[i]()
